import numpy as np
import ml_dtypes


def mxq(x, axis, fmt="e4m3"):
    dtype, down = {"e4m3": (ml_dtypes.float8_e4m3fn, 7), "e5m2": (ml_dtypes.float8_e5m2, 14)}[fmt]
    v = np.moveaxis(np.asarray(x, np.float32).astype(ml_dtypes.bfloat16).astype(np.float64), axis, -1)
    blocks = v.reshape(v.shape[:-1] + (-1, 32))
    amax = np.abs(blocks).max(-1, keepdims=True)
    byte = np.maximum(np.where(amax > 0, np.frexp(amax)[1] - 1 + 127, 0) - down, 1)
    scale = np.exp2(byte - 127.0)
    codes = (blocks / scale).astype(np.float32).astype(dtype).astype(np.float64)
    return np.moveaxis((codes * scale).reshape(v.shape), -1, axis)


WIDE = False


def mx_kscale(k):
    if not WIDE:
        return np.ones(k)
    levels = np.array([10, -10, 5, -5, 0])
    a = np.random.permutation(np.resize(levels, k // 512 * 4)).reshape(k // 512, 4)
    idx = np.arange(k)
    return np.exp2(a[idx // 512, idx % 128 // 32])


BF16 = ml_dtypes.bfloat16


def bf(x):
    return np.asarray(x, np.float32).astype(BF16)


def f64(x):
    return np.asarray(x).astype(np.float64)


B, DS, HH, WW, HID, HL, REP, GRP = 2, 64, 8, 8, 1024, 1024, 8, 4
CO = 2 * GRP * DS


def elu(v):
    return np.where(v > 0.0, v, np.exp(np.minimum(v, 0.0)) - 1.0)


def to_rows(t):
    return t.transpose(0, 2, 3, 1).reshape(B * HH * WW, t.shape[1])


def to_maps(r):
    return r.reshape(B, HH, WW, r.shape[1]).transpose(0, 3, 1, 2)


def setup_inputs():
    s = mx_kscale(HID)
    return {"h3": bf(elu(np.random.standard_normal((B, HID, HH, WW))) * s[None, :, None, None]),
            "w4": bf(np.random.standard_normal((HL, HID)) * 1.2 / np.sqrt(HID) / s[None, :]),
            "w5": bf(np.random.standard_normal((CO, HL)) * 6.0 / np.sqrt(HL))}


def reference(h3, w4, w5):
    h4 = elu(mxq(to_rows(f64(h3)), 1, "e4m3") @ mxq(f64(w4), 1, "e4m3").T)
    f_int = to_maps(mxq(h4, 1, "e4m3") @ mxq(f64(w5), 1, "e4m3").T)
    d4 = GRP * DS
    real = f_int[:, :d4].reshape(B, GRP, DS, HH, WW).mean(axis=1) * 0.1
    imag = f_int[:, d4:].reshape(B, GRP, DS, HH, WW).mean(axis=1) * 0.1
    return np.concatenate([real, imag], axis=1)

@@ -1,0 +1,179 @@
+from contextlib import ExitStack
+
+import concourse.mybir as mybir
+from concourse.masks import make_identity
+
+F32 = mybir.dt.float32
+BF16 = mybir.dt.bfloat16
+U32 = mybir.dt.uint32
+U8 = mybir.dt.uint8
+FP8X4 = mybir.dt.float8_e4m3fn_x4
+ALU = mybir.AluOpType
+ACT = mybir.ActivationFunctionType
+
+P = 128
+PACK = 4
+HALVES = 2
+PAIR = 2
+K = 1024
+PASSES = K // (P * PACK)
+BATCH = 2
+PIXELS_PER_IMAGE = 64
+PIXELS = BATCH * PIXELS_PER_IMAGE
+W4_LOADS = 4
+GROUPS = 4
+PARTS = 2
+D = 64
+SLABS = W4_LOADS * PAIR + GROUPS
+TRANSPOSE_BANKS = 5
+
+FLOPS = 2 * PIXELS * K * K + 2 * PIXELS * K * PARTS * GROUPS * D
+
+
+def transpose_slab(nc, banks, stage, identity, slab_words):
+    bank = banks.tile([P, PASSES, HALVES, P], F32)
+    for g in range(PASSES):
+        for u in range(HALVES):
+            first = (g * HALVES + u) * P
+            nc.tensor.transpose(bank[:, g, u, :], slab_words[:, first : first + P], identity[:])
+    grouped = stage.tile([P, PASSES, P, PACK], BF16, align_bytes=64)
+    nc.scalar.copy(out=grouped[:].bitcast(F32), in_=bank[:].rearrange("q g u r -> q g r u"))
+    return grouped
+
+
+def quantise(nc, grouped, codes, scales):
+    nc.vector.quantize_mx(out=codes.bitcast(FP8X4), scales=scales, in_=grouped)
+
+
+def tile_qca_operator_deep_pb_s_kernel(tc, h3, w4, w5, out):
+    nc = tc.nc
+    with ExitStack() as ctx:
+        keep = ctx.enter_context(tc.tile_pool(name="keep", bufs=1))
+        stage = ctx.enter_context(tc.tile_pool(name="stage", bufs=SLABS))
+        work = ctx.enter_context(tc.tile_pool(name="work", bufs=2))
+        banks = ctx.enter_context(tc.psum_pool(name="banks", bufs=TRANSPOSE_BANKS))
+        h4_banks = ctx.enter_context(tc.psum_pool(name="h4_banks", bufs=2))
+        out_banks = ctx.enter_context(tc.psum_pool(name="out_banks", bufs=1))
+
+        w4_raw = [keep.tile([P, PAIR, K], BF16, name="w4_raw%d" % c) for c in range(W4_LOADS)]
+        w4_rows = w4.rearrange("(c p e) k -> c p e k", p=P, e=PAIR)
+        h3_raw = keep.tile([P, BATCH, PASSES * PACK, PIXELS_PER_IMAGE], BF16)
+        w5_raw = [keep.tile([P, K], BF16, name="w5_raw%d" % g) for g in range(GROUPS)]
+
+        nc.sync.dma_start(out=w4_raw[0][:], in_=w4_rows[0])
+        for b in range(BATCH):
+            nc.sync.dma_start(
+                out=h3_raw[:, b].rearrange("q (c e) x -> q c (e x)", e=PAIR),
+                in_=h3[b].rearrange("(c q e) i j -> q c (e i j)", q=P, e=PAIR),
+            )
+        for c in range(1, W4_LOADS):
+            nc.sync.dma_start(out=w4_raw[c][:], in_=w4_rows[c])
+        for g in range(GROUPS):
+            for h in range(PARTS):
+                first = (h * GROUPS + g) * D
+                nc.sync.dma_start(out=w5_raw[g][h:P:PARTS, :], in_=w5[first : first + D, :])
+
+        identity = keep.tile([P, P], F32)
+        make_identity(nc, identity[:])
+
+        table_warmer = keep.tile([P, 1], F32)
+        nc.vector.memset(table_warmer[:], 0.0)
+        nc.scalar.activation(out=table_warmer[:], in_=table_warmer[:], func=ACT.Exp)
+
+        h3_grouped = keep.tile([P, PASSES, PIXELS, PACK], BF16, align_bytes=64)
+        h3_codes = keep.tile([P, PASSES, PIXELS], U32, align_bytes=64)
+        h3_scales = keep.tile([P, PASSES, PIXELS], U8, align_bytes=64)
+        for g in range(PASSES):
+            nc.vector.tensor_copy(
+                out=h3_grouped[:, g].rearrange("q (b x) t -> q b x t", b=BATCH),
+                in_=h3_raw[:, :, g * PACK : (g + 1) * PACK, :].rearrange("q b t x -> q b x t"),
+            )
+        quantise(
+            nc,
+            h3_grouped[:].rearrange("q g n t -> q (g n t)"),
+            h3_codes[:].rearrange("q g n -> q (g n)"),
+            h3_scales[:].rearrange("q g n -> q (g n)"),
+        )
+
+        h4_grouped = [
+            keep.tile([P, PIXELS, PACK], BF16, name="h4_grouped%d" % g, align_bytes=64)
+            for g in range(PASSES)
+        ]
+        h4_codes = keep.tile([P, PASSES, PIXELS], U32, align_bytes=64)
+        h4_scales = keep.tile([P, PASSES, PIXELS], U8, align_bytes=64)
+        for c in range(W4_LOADS):
+            w4_codes = keep.tile([P, PAIR, PASSES, P], U32, name="w4_codes%d" % c, align_bytes=64)
+            w4_scales = keep.tile([P, PAIR, PASSES, P], U8, name="w4_scales%d" % c, align_bytes=64)
+            w4_words = w4_raw[c][:].bitcast(F32)
+            w4_grouped = [
+                transpose_slab(nc, banks, stage, identity, w4_words[:, e, :]) for e in range(PAIR)
+            ]
+            for e in range(PAIR):
+                quantise(
+                    nc,
+                    w4_grouped[e][:].rearrange("q g r t -> q (g r t)"),
+                    w4_codes[:, e].rearrange("q g r -> q (g r)"),
+                    w4_scales[:, e].rearrange("q g r -> q (g r)"),
+                )
+            h4_sum = h4_banks.tile([P, PAIR, PIXELS], F32)
+            for e in range(PAIR):
+                for g in range(PASSES):
+                    nc.tensor.matmul_mx(
+                        out=h4_sum[:, e, :],
+                        lhsT=w4_codes[:, e, g, :].bitcast(FP8X4),
+                        lhsT_scale=w4_scales[:, e, g, :],
+                        rhs=h3_codes[:, g, :].bitcast(FP8X4),
+                        rhs_scale=h3_scales[:, g, :],
+                        start=(g == 0),
+                        stop=(g == PASSES - 1),
+                    )
+            exp_v = work.tile([P, PAIR, PIXELS], F32)
+            nc.scalar.activation(out=exp_v[:], in_=h4_sum[:], func=ACT.Exp)
+            negative_branch = work.tile([P, PAIR, PIXELS], F32)
+            nc.vector.tensor_scalar(
+                out=negative_branch[:], in0=exp_v[:], scalar1=1.0, scalar2=-1.0, op0=ALU.min, op1=ALU.add
+            )
+            second_pass, u = divmod(c, HALVES)
+            nc.vector.tensor_tensor(
+                out=h4_grouped[second_pass][:, :, u * PAIR : (u + 1) * PAIR],
+                in0=negative_branch[:].rearrange("p e n -> p n e"),
+                in1=h4_sum[:].rearrange("p e n -> p n e"),
+                op=ALU.max,
+            )
+            if u == HALVES - 1:
+                quantise(
+                    nc,
+                    h4_grouped[second_pass][:].rearrange("p n t -> p (n t)"),
+                    h4_codes[:, second_pass, :],
+                    h4_scales[:, second_pass, :],
+                )
+
+        out_sum = out_banks.tile([P, PIXELS], F32)
+        for g in range(GROUPS):
+            w5_codes = keep.tile([P, PASSES, P], U32, name="w5_codes%d" % g, align_bytes=64)
+            w5_scales = keep.tile([P, PASSES, P], U8, name="w5_scales%d" % g, align_bytes=64)
+            w5_grouped = transpose_slab(nc, banks, stage, identity, w5_raw[g][:].bitcast(F32))
+            quantise(
+                nc,
+                w5_grouped[:].rearrange("q g r t -> q (g r t)"),
+                w5_codes[:].rearrange("q g r -> q (g r)"),
+                w5_scales[:].rearrange("q g r -> q (g r)"),
+            )
+            for second_pass in range(PASSES):
+                nc.tensor.matmul_mx(
+                    out=out_sum[:],
+                    lhsT=w5_codes[:, second_pass, :].bitcast(FP8X4),
+                    lhsT_scale=w5_scales[:, second_pass, :],
+                    rhs=h4_codes[:, second_pass, :].bitcast(FP8X4),
+                    rhs_scale=h4_scales[:, second_pass, :],
+                    start=(g == 0 and second_pass == 0),
+                    stop=(g == GROUPS - 1 and second_pass == PASSES - 1),
+                )
+
+        result = keep.tile([P, PIXELS], F32)
+        nc.vector.tensor_scalar_mul(out=result[:], in0=out_sum[:], scalar1=0.1 / GROUPS)
+        for h in range(PARTS):
+            nc.sync.dma_start(
+                out=out[:, h * D : (h + 1) * D].rearrange("b d i j -> d b (i j)"),
+                in_=result[h:P:PARTS, :].rearrange("m (b x) -> m b x", b=BATCH),
+            )

@@ -7,6 +7,7 @@ F32 = mybir.dt.float32
 BF16 = mybir.dt.bfloat16
 U32 = mybir.dt.uint32
 U8 = mybir.dt.uint8
+I32 = mybir.dt.int32
 FP8X4 = mybir.dt.float8_e4m3fn_x4
 ALU = mybir.AluOpType
 ACT = mybir.ActivationFunctionType
@@ -26,6 +27,8 @@ PARTS = 2
 D = 64
 SLABS = W4_LOADS * PAIR + GROUPS
 TRANSPOSE_BANKS = 5
+WARM_UP_COLUMNS = 256
+WARM_UP_PASSES = 10
 
 FLOPS = 2 * PIXELS * K * K + 2 * PIXELS * K * PARTS * GROUPS * D
 
@@ -79,6 +82,23 @@ def tile_qca_operator_deep_pb_s_kernel(tc, h3, w4, w5, out):
         table_warmer = keep.tile([P, 1], F32)
         nc.vector.memset(table_warmer[:], 0.0)
         nc.scalar.activation(out=table_warmer[:], in_=table_warmer[:], func=ACT.Exp)
+
+        zeros = keep.tile([P, WARM_UP_COLUMNS * PACK], BF16, align_bytes=64)
+        zero_codes = keep.tile([P, WARM_UP_COLUMNS], U32, align_bytes=64)
+        zero_scales = keep.tile([P, WARM_UP_COLUMNS], U8, align_bytes=64)
+        nc.vector.memset(zeros[:].bitcast(I32), 0)
+        quantise(nc, zeros[:], zero_codes[:], zero_scales[:])
+        unread = banks.tile([P, WARM_UP_COLUMNS], F32, tag="bank")
+        for i in range(WARM_UP_PASSES):
+            nc.tensor.matmul_mx(
+                out=unread[:],
+                lhsT=zero_codes[:, 0:P].bitcast(FP8X4),
+                lhsT_scale=zero_scales[:, 0:P],
+                rhs=zero_codes[:].bitcast(FP8X4),
+                rhs_scale=zero_scales[:],
+                start=True,
+                stop=True,
+            )
 
         h3_grouped = keep.tile([P, PASSES, PIXELS, PACK], BF16, align_bytes=64)
         h3_codes = keep.tile([P, PASSES, PIXELS], U32, align_bytes=64)

@@ -21,14 +21,15 @@ PASSES = K // (P * PACK)
 BATCH = 2
 PIXELS_PER_IMAGE = 64
 PIXELS = BATCH * PIXELS_PER_IMAGE
+PADDED = 2 * PIXELS
 W4_LOADS = 4
 GROUPS = 4
 PARTS = 2
 D = 64
 SLABS = W4_LOADS * PAIR + GROUPS
 TRANSPOSE_BANKS = 5
-WARM_UP_COLUMNS = 256
 WARM_UP_PASSES = 10
+BRIDGE_PASSES = 4
 
 FLOPS = 2 * PIXELS * K * K + 2 * PIXELS * K * PARTS * GROUPS * D
 
@@ -63,13 +64,12 @@ def tile_qca_operator_deep_pb_s_kernel(tc, h3, w4, w5, out):
         h3_raw = keep.tile([P, BATCH, PASSES * PACK, PIXELS_PER_IMAGE], BF16)
         w5_raw = [keep.tile([P, K], BF16, name="w5_raw%d" % g) for g in range(GROUPS)]
 
-        nc.sync.dma_start(out=w4_raw[0][:], in_=w4_rows[0])
         for b in range(BATCH):
             nc.sync.dma_start(
                 out=h3_raw[:, b].rearrange("q (c e) x -> q c (e x)", e=PAIR),
                 in_=h3[b].rearrange("(c q e) i j -> q c (e i j)", q=P, e=PAIR),
             )
-        for c in range(1, W4_LOADS):
+        for c in range(W4_LOADS):
             nc.sync.dma_start(out=w4_raw[c][:], in_=w4_rows[c])
         for g in range(GROUPS):
             for h in range(PARTS):
@@ -83,37 +83,46 @@ def tile_qca_operator_deep_pb_s_kernel(tc, h3, w4, w5, out):
         nc.vector.memset(table_warmer[:], 0.0)
         nc.scalar.activation(out=table_warmer[:], in_=table_warmer[:], func=ACT.Exp)
 
-        zeros = keep.tile([P, WARM_UP_COLUMNS * PACK], BF16, align_bytes=64)
-        zero_codes = keep.tile([P, WARM_UP_COLUMNS], U32, align_bytes=64)
-        zero_scales = keep.tile([P, WARM_UP_COLUMNS], U8, align_bytes=64)
+        zeros = keep.tile([P, PADDED * PACK], BF16, align_bytes=64)
+        zero_codes = keep.tile([P, PADDED], U32, align_bytes=64)
+        zero_scales = keep.tile([P, PADDED], U8, align_bytes=64)
         nc.vector.memset(zeros[:].bitcast(I32), 0)
         quantise(nc, zeros[:], zero_codes[:], zero_scales[:])
-        unread = banks.tile([P, WARM_UP_COLUMNS], F32, tag="bank")
-        for i in range(WARM_UP_PASSES):
-            nc.tensor.matmul_mx(
-                out=unread[:],
-                lhsT=zero_codes[:, 0:P].bitcast(FP8X4),
-                lhsT_scale=zero_scales[:, 0:P],
-                rhs=zero_codes[:].bitcast(FP8X4),
-                rhs_scale=zero_scales[:],
-                start=True,
-                stop=True,
-            )
+
+        def stream_unread_columns(passes, codes, scales):
+            unread = banks.tile([P, PADDED], F32, tag="bank")
+            for i in range(passes):
+                nc.tensor.matmul_mx(
+                    out=unread[:],
+                    lhsT=zero_codes[:, 0:P].bitcast(FP8X4),
+                    lhsT_scale=zero_scales[:, 0:P],
+                    rhs=codes.bitcast(FP8X4),
+                    rhs_scale=scales,
+                    start=True,
+                    stop=True,
+                )
+
+        stream_unread_columns(WARM_UP_PASSES, zero_codes[:], zero_scales[:])
 
         h3_grouped = keep.tile([P, PASSES, PIXELS, PACK], BF16, align_bytes=64)
-        h3_codes = keep.tile([P, PASSES, PIXELS], U32, align_bytes=64)
-        h3_scales = keep.tile([P, PASSES, PIXELS], U8, align_bytes=64)
+        h3_codes = keep.tile([P, PASSES, PADDED], U32, align_bytes=64)
+        h3_scales = keep.tile([P, PASSES, PADDED], U8, align_bytes=64)
+        for g in range(PASSES):
+            quantise(
+                nc, zeros[:, 0 : PIXELS * PACK], h3_codes[:, g, PIXELS:PADDED], h3_scales[:, g, PIXELS:PADDED]
+            )
         for g in range(PASSES):
             nc.vector.tensor_copy(
                 out=h3_grouped[:, g].rearrange("q (b x) t -> q b x t", b=BATCH),
                 in_=h3_raw[:, :, g * PACK : (g + 1) * PACK, :].rearrange("q b t x -> q b x t"),
             )
-        quantise(
-            nc,
-            h3_grouped[:].rearrange("q g n t -> q (g n t)"),
-            h3_codes[:].rearrange("q g n -> q (g n)"),
-            h3_scales[:].rearrange("q g n -> q (g n)"),
-        )
+        for g in range(PASSES):
+            quantise(
+                nc,
+                h3_grouped[:, g].rearrange("q n t -> q (n t)"),
+                h3_codes[:, g, 0:PIXELS],
+                h3_scales[:, g, 0:PIXELS],
+            )
 
         h4_grouped = [
             keep.tile([P, PIXELS, PACK], BF16, name="h4_grouped%d" % g, align_bytes=64)
@@ -128,6 +137,8 @@ def tile_qca_operator_deep_pb_s_kernel(tc, h3, w4, w5, out):
             w4_grouped = [
                 transpose_slab(nc, banks, stage, identity, w4_words[:, e, :]) for e in range(PAIR)
             ]
+            if c == 0:
+                stream_unread_columns(BRIDGE_PASSES, h3_codes[:, 0, :], h3_scales[:, 0, :])
             for e in range(PAIR):
                 quantise(
                     nc,
@@ -135,7 +146,7 @@ def tile_qca_operator_deep_pb_s_kernel(tc, h3, w4, w5, out):
                     w4_codes[:, e].rearrange("q g r -> q (g r)"),
                     w4_scales[:, e].rearrange("q g r -> q (g r)"),
                 )
-            h4_sum = h4_banks.tile([P, PAIR, PIXELS], F32)
+            h4_sum = h4_banks.tile([P, PAIR, PADDED], F32)
             for e in range(PAIR):
                 for g in range(PASSES):
                     nc.tensor.matmul_mx(
@@ -148,7 +159,7 @@ def tile_qca_operator_deep_pb_s_kernel(tc, h3, w4, w5, out):
                         stop=(g == PASSES - 1),
                     )
             exp_v = work.tile([P, PAIR, PIXELS], F32)
-            nc.scalar.activation(out=exp_v[:], in_=h4_sum[:], func=ACT.Exp)
+            nc.scalar.activation(out=exp_v[:], in_=h4_sum[:, :, 0:PIXELS], func=ACT.Exp)
             negative_branch = work.tile([P, PAIR, PIXELS], F32)
             nc.vector.tensor_scalar(
                 out=negative_branch[:], in0=exp_v[:], scalar1=1.0, scalar2=-1.0, op0=ALU.min, op1=ALU.add
@@ -157,7 +168,7 @@ def tile_qca_operator_deep_pb_s_kernel(tc, h3, w4, w5, out):
             nc.vector.tensor_tensor(
                 out=h4_grouped[second_pass][:, :, u * PAIR : (u + 1) * PAIR],
                 in0=negative_branch[:].rearrange("p e n -> p n e"),
-                in1=h4_sum[:].rearrange("p e n -> p n e"),
+                in1=h4_sum[:, :, 0:PIXELS].rearrange("p e n -> p n e"),
                 op=ALU.max,
             )
             if u == HALVES - 1:

@@ -21,60 +21,56 @@ PASSES = K // (P * PACK)
 BATCH = 2
 PIXELS_PER_IMAGE = 64
 PIXELS = BATCH * PIXELS_PER_IMAGE
-PADDED = 2 * PIXELS
 W4_LOADS = 4
 GROUPS = 4
 PARTS = 2
 D = 64
 SLABS = W4_LOADS * PAIR + GROUPS
 TRANSPOSE_BANKS = 5
+UNREAD_COLUMNS = 256
 WARM_UP_PASSES = 10
-BRIDGE_PASSES = 4
+BRIDGE_PASSES = 6
+PRODUCT_LAG = 4
+ELU_STEPS = 3
 
 FLOPS = 2 * PIXELS * K * K + 2 * PIXELS * K * PARTS * GROUPS * D
-
-
-def transpose_slab(nc, banks, stage, identity, slab_words):
-    bank = banks.tile([P, PASSES, HALVES, P], F32)
-    for g in range(PASSES):
-        for u in range(HALVES):
-            first = (g * HALVES + u) * P
-            nc.tensor.transpose(bank[:, g, u, :], slab_words[:, first : first + P], identity[:])
-    grouped = stage.tile([P, PASSES, P, PACK], BF16, align_bytes=64)
-    nc.scalar.copy(out=grouped[:].bitcast(F32), in_=bank[:].rearrange("q g u r -> q g r u"))
-    return grouped
-
-
-def quantise(nc, grouped, codes, scales):
-    nc.vector.quantize_mx(out=codes.bitcast(FP8X4), scales=scales, in_=grouped)
 
 
 def tile_qca_operator_deep_pb_s_kernel(tc, h3, w4, w5, out):
     nc = tc.nc
     with ExitStack() as ctx:
         keep = ctx.enter_context(tc.tile_pool(name="keep", bufs=1))
-        stage = ctx.enter_context(tc.tile_pool(name="stage", bufs=SLABS))
         work = ctx.enter_context(tc.tile_pool(name="work", bufs=2))
         banks = ctx.enter_context(tc.psum_pool(name="banks", bufs=TRANSPOSE_BANKS))
         h4_banks = ctx.enter_context(tc.psum_pool(name="h4_banks", bufs=2))
         out_banks = ctx.enter_context(tc.psum_pool(name="out_banks", bufs=1))
+        ctx.enter_context(tc.manual_schedule())
 
         w4_raw = [keep.tile([P, PAIR, K], BF16, name="w4_raw%d" % c) for c in range(W4_LOADS)]
         w4_rows = w4.rearrange("(c p e) k -> c p e k", p=P, e=PAIR)
         h3_raw = keep.tile([P, BATCH, PASSES * PACK, PIXELS_PER_IMAGE], BF16)
         w5_raw = [keep.tile([P, K], BF16, name="w5_raw%d" % g) for g in range(GROUPS)]
 
+        nc.sync.dma_start(out=w4_raw[0][:], in_=w4_rows[0])
         for b in range(BATCH):
             nc.sync.dma_start(
                 out=h3_raw[:, b].rearrange("q (c e) x -> q c (e x)", e=PAIR),
                 in_=h3[b].rearrange("(c q e) i j -> q c (e i j)", q=P, e=PAIR),
             )
-        for c in range(W4_LOADS):
+        for c in range(1, W4_LOADS):
             nc.sync.dma_start(out=w4_raw[c][:], in_=w4_rows[c])
         for g in range(GROUPS):
             for h in range(PARTS):
                 first = (h * GROUPS + g) * D
                 nc.sync.dma_start(out=w5_raw[g][h:P:PARTS, :], in_=w5[first : first + D, :])
+
+        slab_words = [w4_raw[c][:].bitcast(F32)[:, e, :] for c in range(W4_LOADS) for e in range(PAIR)]
+        slab_words.extend([w5_raw[g][:].bitcast(F32) for g in range(GROUPS)])
+        grouped = [
+            keep.tile([P, PASSES, P, PACK], BF16, name="grouped%d" % s, align_bytes=64) for s in range(SLABS)
+        ]
+        codes = [keep.tile([P, PASSES, P], U32, name="codes%d" % s, align_bytes=64) for s in range(SLABS)]
+        scales = [keep.tile([P, PASSES, P], U8, name="scales%d" % s, align_bytes=64) for s in range(SLABS)]
 
         identity = keep.tile([P, P], F32)
         make_identity(nc, identity[:])
@@ -83,46 +79,40 @@ def tile_qca_operator_deep_pb_s_kernel(tc, h3, w4, w5, out):
         nc.vector.memset(table_warmer[:], 0.0)
         nc.scalar.activation(out=table_warmer[:], in_=table_warmer[:], func=ACT.Exp)
 
-        zeros = keep.tile([P, PADDED * PACK], BF16, align_bytes=64)
-        zero_codes = keep.tile([P, PADDED], U32, align_bytes=64)
-        zero_scales = keep.tile([P, PADDED], U8, align_bytes=64)
+        zeros = keep.tile([P, UNREAD_COLUMNS * PACK], BF16, align_bytes=64)
+        zero_codes = keep.tile([P, UNREAD_COLUMNS], U32, align_bytes=64)
+        zero_scales = keep.tile([P, UNREAD_COLUMNS], U8, align_bytes=64)
         nc.vector.memset(zeros[:].bitcast(I32), 0)
-        quantise(nc, zeros[:], zero_codes[:], zero_scales[:])
+        nc.vector.quantize_mx(out=zero_codes[:].bitcast(FP8X4), scales=zero_scales[:], in_=zeros[:])
 
-        def stream_unread_columns(passes, codes, scales):
-            unread = banks.tile([P, PADDED], F32, tag="bank")
+        def multiply_zeros(passes):
+            unread = banks.tile([P, UNREAD_COLUMNS], F32, tag="bank")
             for i in range(passes):
                 nc.tensor.matmul_mx(
                     out=unread[:],
                     lhsT=zero_codes[:, 0:P].bitcast(FP8X4),
                     lhsT_scale=zero_scales[:, 0:P],
-                    rhs=codes.bitcast(FP8X4),
-                    rhs_scale=scales,
+                    rhs=zero_codes[:].bitcast(FP8X4),
+                    rhs_scale=zero_scales[:],
                     start=True,
                     stop=True,
                 )
 
-        stream_unread_columns(WARM_UP_PASSES, zero_codes[:], zero_scales[:])
+        multiply_zeros(WARM_UP_PASSES)
 
         h3_grouped = keep.tile([P, PASSES, PIXELS, PACK], BF16, align_bytes=64)
-        h3_codes = keep.tile([P, PASSES, PADDED], U32, align_bytes=64)
-        h3_scales = keep.tile([P, PASSES, PADDED], U8, align_bytes=64)
-        for g in range(PASSES):
-            quantise(
-                nc, zeros[:, 0 : PIXELS * PACK], h3_codes[:, g, PIXELS:PADDED], h3_scales[:, g, PIXELS:PADDED]
-            )
+        h3_codes = keep.tile([P, PASSES, PIXELS], U32, align_bytes=64)
+        h3_scales = keep.tile([P, PASSES, PIXELS], U8, align_bytes=64)
         for g in range(PASSES):
             nc.vector.tensor_copy(
                 out=h3_grouped[:, g].rearrange("q (b x) t -> q b x t", b=BATCH),
                 in_=h3_raw[:, :, g * PACK : (g + 1) * PACK, :].rearrange("q b t x -> q b x t"),
             )
-        for g in range(PASSES):
-            quantise(
-                nc,
-                h3_grouped[:, g].rearrange("q n t -> q (n t)"),
-                h3_codes[:, g, 0:PIXELS],
-                h3_scales[:, g, 0:PIXELS],
-            )
+        nc.vector.quantize_mx(
+            out=h3_codes[:].rearrange("q g n -> q (g n)").bitcast(FP8X4),
+            scales=h3_scales[:].rearrange("q g n -> q (g n)"),
+            in_=h3_grouped[:].rearrange("q g n t -> q (g n t)"),
+        )
 
         h4_grouped = [
             keep.tile([P, PIXELS, PACK], BF16, name="h4_grouped%d" % g, align_bytes=64)
@@ -130,71 +120,91 @@ def tile_qca_operator_deep_pb_s_kernel(tc, h3, w4, w5, out):
         ]
         h4_codes = keep.tile([P, PASSES, PIXELS], U32, align_bytes=64)
         h4_scales = keep.tile([P, PASSES, PIXELS], U8, align_bytes=64)
-        for c in range(W4_LOADS):
-            w4_codes = keep.tile([P, PAIR, PASSES, P], U32, name="w4_codes%d" % c, align_bytes=64)
-            w4_scales = keep.tile([P, PAIR, PASSES, P], U8, name="w4_scales%d" % c, align_bytes=64)
-            w4_words = w4_raw[c][:].bitcast(F32)
-            w4_grouped = [
-                transpose_slab(nc, banks, stage, identity, w4_words[:, e, :]) for e in range(PAIR)
-            ]
-            if c == 0:
-                stream_unread_columns(BRIDGE_PASSES, h3_codes[:, 0, :], h3_scales[:, 0, :])
-            for e in range(PAIR):
-                quantise(
-                    nc,
-                    w4_grouped[e][:].rearrange("q g r t -> q (g r t)"),
-                    w4_codes[:, e].rearrange("q g r -> q (g r)"),
-                    w4_scales[:, e].rearrange("q g r -> q (g r)"),
-                )
-            h4_sum = h4_banks.tile([P, PAIR, PADDED], F32)
+        h4_sums = {}
+        exp_v = {}
+        negative_branch = {}
+
+        def transpose_and_copy(s):
+            bank = banks.tile([P, PASSES, HALVES, P], F32)
+            for g in range(PASSES):
+                for u in range(HALVES):
+                    first = (g * HALVES + u) * P
+                    nc.tensor.transpose(bank[:, g, u, :], slab_words[s][:, first : first + P], identity[:])
+            nc.scalar.copy(out=grouped[s][:].bitcast(F32), in_=bank[:].rearrange("q g u r -> q g r u"))
+
+        def quantise_slab(s):
+            nc.vector.quantize_mx(
+                out=codes[s][:].rearrange("q g r -> q (g r)").bitcast(FP8X4),
+                scales=scales[s][:].rearrange("q g r -> q (g r)"),
+                in_=grouped[s][:].rearrange("q g r t -> q (g r t)"),
+            )
+
+        def first_layer_and_exp(c):
+            h4_sums[c] = h4_banks.tile([P, PAIR, PIXELS], F32, name="h4_sum")
             for e in range(PAIR):
                 for g in range(PASSES):
                     nc.tensor.matmul_mx(
-                        out=h4_sum[:, e, :],
-                        lhsT=w4_codes[:, e, g, :].bitcast(FP8X4),
-                        lhsT_scale=w4_scales[:, e, g, :],
+                        out=h4_sums[c][:, e, :],
+                        lhsT=codes[c * PAIR + e][:, g, :].bitcast(FP8X4),
+                        lhsT_scale=scales[c * PAIR + e][:, g, :],
                         rhs=h3_codes[:, g, :].bitcast(FP8X4),
                         rhs_scale=h3_scales[:, g, :],
                         start=(g == 0),
                         stop=(g == PASSES - 1),
                     )
-            exp_v = work.tile([P, PAIR, PIXELS], F32)
-            nc.scalar.activation(out=exp_v[:], in_=h4_sum[:, :, 0:PIXELS], func=ACT.Exp)
-            negative_branch = work.tile([P, PAIR, PIXELS], F32)
+            exp_v[c] = work.tile([P, PAIR, PIXELS], F32, name="exp_v")
+            nc.scalar.activation(out=exp_v[c][:], in_=h4_sums[c][:], func=ACT.Exp)
+
+        def negative_branch_of_elu(c):
+            negative_branch[c] = work.tile([P, PAIR, PIXELS], F32, name="negative_branch")
             nc.vector.tensor_scalar(
-                out=negative_branch[:], in0=exp_v[:], scalar1=1.0, scalar2=-1.0, op0=ALU.min, op1=ALU.add
+                out=negative_branch[c][:], in0=exp_v[c][:], scalar1=1.0, scalar2=-1.0, op0=ALU.min, op1=ALU.add
             )
+
+        def finish_elu(c):
             second_pass, u = divmod(c, HALVES)
             nc.vector.tensor_tensor(
                 out=h4_grouped[second_pass][:, :, u * PAIR : (u + 1) * PAIR],
-                in0=negative_branch[:].rearrange("p e n -> p n e"),
-                in1=h4_sum[:, :, 0:PIXELS].rearrange("p e n -> p n e"),
+                in0=negative_branch[c][:].rearrange("p e n -> p n e"),
+                in1=h4_sums[c][:].rearrange("p e n -> p n e"),
                 op=ALU.max,
             )
-            if u == HALVES - 1:
-                quantise(
-                    nc,
-                    h4_grouped[second_pass][:].rearrange("p n t -> p (n t)"),
-                    h4_codes[:, second_pass, :],
-                    h4_scales[:, second_pass, :],
-                )
+
+        def quantise_h4(second_pass):
+            nc.vector.quantize_mx(
+                out=h4_codes[:, second_pass, :].bitcast(FP8X4),
+                scales=h4_scales[:, second_pass, :],
+                in_=h4_grouped[second_pass][:].rearrange("p n t -> p (n t)"),
+            )
+
+        for s in range(SLABS + ELU_STEPS):
+            if s < SLABS:
+                transpose_and_copy(s)
+            if s == PAIR - 1:
+                multiply_zeros(BRIDGE_PASSES)
+            if 1 <= s <= SLABS:
+                quantise_slab(s - 1)
+            for step in range(ELU_STEPS + 1):
+                c, odd = divmod(s - PRODUCT_LAG - step, PAIR)
+                if odd or not 0 <= c < W4_LOADS:
+                    continue
+                if step == 0:
+                    first_layer_and_exp(c)
+                if step == 1:
+                    negative_branch_of_elu(c)
+                if step == 2:
+                    finish_elu(c)
+                if step == 3 and c % HALVES == HALVES - 1:
+                    quantise_h4(c // HALVES)
 
         out_sum = out_banks.tile([P, PIXELS], F32)
         for g in range(GROUPS):
-            w5_codes = keep.tile([P, PASSES, P], U32, name="w5_codes%d" % g, align_bytes=64)
-            w5_scales = keep.tile([P, PASSES, P], U8, name="w5_scales%d" % g, align_bytes=64)
-            w5_grouped = transpose_slab(nc, banks, stage, identity, w5_raw[g][:].bitcast(F32))
-            quantise(
-                nc,
-                w5_grouped[:].rearrange("q g r t -> q (g r t)"),
-                w5_codes[:].rearrange("q g r -> q (g r)"),
-                w5_scales[:].rearrange("q g r -> q (g r)"),
-            )
+            s = W4_LOADS * PAIR + g
             for second_pass in range(PASSES):
                 nc.tensor.matmul_mx(
                     out=out_sum[:],
-                    lhsT=w5_codes[:, second_pass, :].bitcast(FP8X4),
-                    lhsT_scale=w5_scales[:, second_pass, :],
+                    lhsT=codes[s][:, second_pass, :].bitcast(FP8X4),
+                    lhsT_scale=scales[s][:, second_pass, :],
                     rhs=h4_codes[:, second_pass, :].bitcast(FP8X4),
                     rhs_scale=h4_scales[:, second_pass, :],
                     start=(g == 0 and second_pass == 0),

@@ -7,7 +7,6 @@ F32 = mybir.dt.float32
 BF16 = mybir.dt.bfloat16
 U32 = mybir.dt.uint32
 U8 = mybir.dt.uint8
-I32 = mybir.dt.int32
 FP8X4 = mybir.dt.float8_e4m3fn_x4
 ALU = mybir.AluOpType
 ACT = mybir.ActivationFunctionType
@@ -27,9 +26,6 @@ PARTS = 2
 D = 64
 SLABS = W4_LOADS * PAIR + GROUPS
 TRANSPOSE_BANKS = 5
-UNREAD_COLUMNS = 256
-WARM_UP_PASSES = 10
-BRIDGE_PASSES = 6
 PRODUCT_LAG = 4
 ELU_STEPS = 3
 
@@ -78,27 +74,6 @@ def tile_qca_operator_deep_pb_s_kernel(tc, h3, w4, w5, out):
         table_warmer = keep.tile([P, 1], F32)
         nc.vector.memset(table_warmer[:], 0.0)
         nc.scalar.activation(out=table_warmer[:], in_=table_warmer[:], func=ACT.Exp)
-
-        zeros = keep.tile([P, UNREAD_COLUMNS * PACK], BF16, align_bytes=64)
-        zero_codes = keep.tile([P, UNREAD_COLUMNS], U32, align_bytes=64)
-        zero_scales = keep.tile([P, UNREAD_COLUMNS], U8, align_bytes=64)
-        nc.vector.memset(zeros[:].bitcast(I32), 0)
-        nc.vector.quantize_mx(out=zero_codes[:].bitcast(FP8X4), scales=zero_scales[:], in_=zeros[:])
-
-        def multiply_zeros(passes):
-            unread = banks.tile([P, UNREAD_COLUMNS], F32, tag="bank")
-            for i in range(passes):
-                nc.tensor.matmul_mx(
-                    out=unread[:],
-                    lhsT=zero_codes[:, 0:P].bitcast(FP8X4),
-                    lhsT_scale=zero_scales[:, 0:P],
-                    rhs=zero_codes[:].bitcast(FP8X4),
-                    rhs_scale=zero_scales[:],
-                    start=True,
-                    stop=True,
-                )
-
-        multiply_zeros(WARM_UP_PASSES)
 
         h3_grouped = keep.tile([P, PASSES, PIXELS, PACK], BF16, align_bytes=64)
         h3_codes = keep.tile([P, PASSES, PIXELS], U32, align_bytes=64)
@@ -180,8 +155,6 @@ def tile_qca_operator_deep_pb_s_kernel(tc, h3, w4, w5, out):
         for s in range(SLABS + ELU_STEPS):
             if s < SLABS:
                 transpose_and_copy(s)
-            if s == PAIR - 1:
-                multiply_zeros(BRIDGE_PASSES)
             if 1 <= s <= SLABS:
                 quantise_slab(s - 1)
             for step in range(ELU_STEPS + 1):

@@ -7,6 +7,7 @@ F32 = mybir.dt.float32
 BF16 = mybir.dt.bfloat16
 U32 = mybir.dt.uint32
 U8 = mybir.dt.uint8
+I32 = mybir.dt.int32
 FP8X4 = mybir.dt.float8_e4m3fn_x4
 ALU = mybir.AluOpType
 ACT = mybir.ActivationFunctionType
@@ -25,9 +26,12 @@ GROUPS = 4
 PARTS = 2
 D = 64
 SLABS = W4_LOADS * PAIR + GROUPS
+SLAB_PAIRS = SLABS // 2
 TRANSPOSE_BANKS = 5
-PRODUCT_LAG = 4
-ELU_STEPS = 3
+UNREAD_COLUMNS = 256
+WARM_UP_PASSES = 10
+BRIDGE_PASSES = 6
+LOAD_LAG = 2
 
 FLOPS = 2 * PIXELS * K * K + 2 * PIXELS * K * PARTS * GROUPS * D
 
@@ -36,9 +40,8 @@ def tile_qca_operator_deep_pb_s_kernel(tc, h3, w4, w5, out):
     nc = tc.nc
     with ExitStack() as ctx:
         keep = ctx.enter_context(tc.tile_pool(name="keep", bufs=1))
-        work = ctx.enter_context(tc.tile_pool(name="work", bufs=2))
         banks = ctx.enter_context(tc.psum_pool(name="banks", bufs=TRANSPOSE_BANKS))
-        h4_banks = ctx.enter_context(tc.psum_pool(name="h4_banks", bufs=2))
+        h4_banks = ctx.enter_context(tc.psum_pool(name="h4_banks", bufs=1))
         out_banks = ctx.enter_context(tc.psum_pool(name="out_banks", bufs=1))
         ctx.enter_context(tc.manual_schedule())
 
@@ -57,8 +60,8 @@ def tile_qca_operator_deep_pb_s_kernel(tc, h3, w4, w5, out):
             nc.sync.dma_start(out=w4_raw[c][:], in_=w4_rows[c])
         for g in range(GROUPS):
             for h in range(PARTS):
-                first = (h * GROUPS + g) * D
-                nc.sync.dma_start(out=w5_raw[g][h:P:PARTS, :], in_=w5[first : first + D, :])
+                first_row = (h * GROUPS + g) * D
+                nc.sync.dma_start(out=w5_raw[g][h:P:PARTS, :], in_=w5[first_row : first_row + D, :])
 
         slab_words = [w4_raw[c][:].bitcast(F32)[:, e, :] for c in range(W4_LOADS) for e in range(PAIR)]
         slab_words.extend([w5_raw[g][:].bitcast(F32) for g in range(GROUPS)])
@@ -75,73 +78,102 @@ def tile_qca_operator_deep_pb_s_kernel(tc, h3, w4, w5, out):
         nc.vector.memset(table_warmer[:], 0.0)
         nc.scalar.activation(out=table_warmer[:], in_=table_warmer[:], func=ACT.Exp)
 
+        zeros = keep.tile([P, UNREAD_COLUMNS * PACK], BF16, align_bytes=64)
+        zero_codes = keep.tile([P, UNREAD_COLUMNS], U32, align_bytes=64)
+        zero_scales = keep.tile([P, UNREAD_COLUMNS], U8, align_bytes=64)
+        nc.vector.memset(zeros[:].bitcast(I32), 0)
+        nc.vector.quantize_mx(out=zero_codes[:].bitcast(FP8X4), scales=zero_scales[:], in_=zeros[:])
+
+        def multiply_zeros(passes):
+            unread = banks.tile([P, UNREAD_COLUMNS], F32, tag="bank")
+            for i in range(passes):
+                nc.tensor.matmul_mx(
+                    out=unread[:],
+                    lhsT=zero_codes[:, 0:P].bitcast(FP8X4),
+                    lhsT_scale=zero_scales[:, 0:P],
+                    rhs=zero_codes[:].bitcast(FP8X4),
+                    rhs_scale=zero_scales[:],
+                    start=True,
+                    stop=True,
+                )
+
+        multiply_zeros(WARM_UP_PASSES)
+
         h3_grouped = keep.tile([P, PASSES, PIXELS, PACK], BF16, align_bytes=64)
         h3_codes = keep.tile([P, PASSES, PIXELS], U32, align_bytes=64)
         h3_scales = keep.tile([P, PASSES, PIXELS], U8, align_bytes=64)
-        for g in range(PASSES):
+        for a in range(PASSES):
             nc.vector.tensor_copy(
-                out=h3_grouped[:, g].rearrange("q (b x) t -> q b x t", b=BATCH),
-                in_=h3_raw[:, :, g * PACK : (g + 1) * PACK, :].rearrange("q b t x -> q b x t"),
+                out=h3_grouped[:, a].rearrange("q (b x) t -> q b x t", b=BATCH),
+                in_=h3_raw[:, :, a * PACK : (a + 1) * PACK, :].rearrange("q b t x -> q b x t"),
             )
         nc.vector.quantize_mx(
-            out=h3_codes[:].rearrange("q g n -> q (g n)").bitcast(FP8X4),
-            scales=h3_scales[:].rearrange("q g n -> q (g n)"),
-            in_=h3_grouped[:].rearrange("q g n t -> q (g n t)"),
+            out=h3_codes[:].rearrange("q a n -> q (a n)").bitcast(FP8X4),
+            scales=h3_scales[:].rearrange("q a n -> q (a n)"),
+            in_=h3_grouped[:].rearrange("q a n t -> q (a n t)"),
         )
 
+        h4_sum = [h4_banks.tile([P, PACK, PIXELS], F32, name="h4_sum%d" % a) for a in range(PASSES)]
+        exp_v = [keep.tile([P, PACK, PIXELS], F32, name="exp_v%d" % a) for a in range(PASSES)]
+        negative = [keep.tile([P, PACK, PIXELS], F32, name="negative%d" % a) for a in range(PASSES)]
         h4_grouped = [
-            keep.tile([P, PIXELS, PACK], BF16, name="h4_grouped%d" % g, align_bytes=64)
-            for g in range(PASSES)
+            keep.tile([P, PIXELS, PACK], BF16, name="h4_grouped%d" % a, align_bytes=64) for a in range(PASSES)
         ]
         h4_codes = keep.tile([P, PASSES, PIXELS], U32, align_bytes=64)
         h4_scales = keep.tile([P, PASSES, PIXELS], U8, align_bytes=64)
-        h4_sums = {}
-        exp_v = {}
-        negative_branch = {}
 
         def transpose_and_copy(s):
             bank = banks.tile([P, PASSES, HALVES, P], F32)
-            for g in range(PASSES):
+            for a in range(PASSES):
                 for u in range(HALVES):
-                    first = (g * HALVES + u) * P
-                    nc.tensor.transpose(bank[:, g, u, :], slab_words[s][:, first : first + P], identity[:])
-            nc.scalar.copy(out=grouped[s][:].bitcast(F32), in_=bank[:].rearrange("q g u r -> q g r u"))
+                    first_word = (a * HALVES + u) * P
+                    nc.tensor.transpose(
+                        bank[:, a, u, :], slab_words[s][:, first_word : first_word + P], identity[:]
+                    )
+            nc.scalar.copy(out=grouped[s][:].bitcast(F32), in_=bank[:].rearrange("q a u r -> q a r u"))
 
         def quantise_slab(s):
             nc.vector.quantize_mx(
-                out=codes[s][:].rearrange("q g r -> q (g r)").bitcast(FP8X4),
-                scales=scales[s][:].rearrange("q g r -> q (g r)"),
-                in_=grouped[s][:].rearrange("q g r t -> q (g r t)"),
+                out=codes[s][:].rearrange("q a r -> q (a r)").bitcast(FP8X4),
+                scales=scales[s][:].rearrange("q a r -> q (a r)"),
+                in_=grouped[s][:].rearrange("q a r t -> q (a r t)"),
             )
 
         def first_layer_and_exp(c):
-            h4_sums[c] = h4_banks.tile([P, PAIR, PIXELS], F32, name="h4_sum")
+            second_pass, u = divmod(c, HALVES)
+            values = slice(u * PAIR, (u + 1) * PAIR)
             for e in range(PAIR):
-                for g in range(PASSES):
+                for a in range(PASSES):
                     nc.tensor.matmul_mx(
-                        out=h4_sums[c][:, e, :],
-                        lhsT=codes[c * PAIR + e][:, g, :].bitcast(FP8X4),
-                        lhsT_scale=scales[c * PAIR + e][:, g, :],
-                        rhs=h3_codes[:, g, :].bitcast(FP8X4),
-                        rhs_scale=h3_scales[:, g, :],
-                        start=(g == 0),
-                        stop=(g == PASSES - 1),
+                        out=h4_sum[second_pass][:, u * PAIR + e, :],
+                        lhsT=codes[c * PAIR + e][:, a, :].bitcast(FP8X4),
+                        lhsT_scale=scales[c * PAIR + e][:, a, :],
+                        rhs=h3_codes[:, a, :].bitcast(FP8X4),
+                        rhs_scale=h3_scales[:, a, :],
+                        start=(a == 0),
+                        stop=(a == PASSES - 1),
                     )
-            exp_v[c] = work.tile([P, PAIR, PIXELS], F32, name="exp_v")
-            nc.scalar.activation(out=exp_v[c][:], in_=h4_sums[c][:], func=ACT.Exp)
-
-        def negative_branch_of_elu(c):
-            negative_branch[c] = work.tile([P, PAIR, PIXELS], F32, name="negative_branch")
-            nc.vector.tensor_scalar(
-                out=negative_branch[c][:], in0=exp_v[c][:], scalar1=1.0, scalar2=-1.0, op0=ALU.min, op1=ALU.add
+            nc.scalar.activation(
+                out=exp_v[second_pass][:, values, :], in_=h4_sum[second_pass][:, values, :], func=ACT.Exp
             )
 
-        def finish_elu(c):
+        def negative_branch(c):
             second_pass, u = divmod(c, HALVES)
+            values = slice(u * PAIR, (u + 1) * PAIR)
+            nc.vector.tensor_scalar(
+                out=negative[second_pass][:, values, :],
+                in0=exp_v[second_pass][:, values, :],
+                scalar1=1.0,
+                scalar2=-1.0,
+                op0=ALU.min,
+                op1=ALU.add,
+            )
+
+        def finish_elu(second_pass):
             nc.vector.tensor_tensor(
-                out=h4_grouped[second_pass][:, :, u * PAIR : (u + 1) * PAIR],
-                in0=negative_branch[c][:].rearrange("p e n -> p n e"),
-                in1=h4_sums[c][:].rearrange("p e n -> p n e"),
+                out=h4_grouped[second_pass][:],
+                in0=negative[second_pass][:].rearrange("p t n -> p n t"),
+                in1=h4_sum[second_pass][:].rearrange("p t n -> p n t"),
                 op=ALU.max,
             )
 
@@ -152,36 +184,38 @@ def tile_qca_operator_deep_pb_s_kernel(tc, h3, w4, w5, out):
                 in_=h4_grouped[second_pass][:].rearrange("p n t -> p (n t)"),
             )
 
-        for s in range(SLABS + ELU_STEPS):
-            if s < SLABS:
-                transpose_and_copy(s)
-            if 1 <= s <= SLABS:
-                quantise_slab(s - 1)
-            for step in range(ELU_STEPS + 1):
-                c, odd = divmod(s - PRODUCT_LAG - step, PAIR)
-                if odd or not 0 <= c < W4_LOADS:
-                    continue
-                if step == 0:
-                    first_layer_and_exp(c)
-                if step == 1:
-                    negative_branch_of_elu(c)
-                if step == 2:
-                    finish_elu(c)
-                if step == 3 and c % HALVES == HALVES - 1:
-                    quantise_h4(c // HALVES)
+        for i in range(SLAB_PAIRS + 1):
+            c = i - LOAD_LAG
+            if i < SLAB_PAIRS:
+                transpose_and_copy(2 * i)
+            if i >= 1:
+                quantise_slab(2 * i - 1)
+                if c >= 1 and (c - 1) % HALVES == HALVES - 1:
+                    quantise_h4((c - 1) // HALVES)
+            if 0 <= c < W4_LOADS:
+                first_layer_and_exp(c)
+            if i < SLAB_PAIRS:
+                transpose_and_copy(2 * i + 1)
+                if i == 0:
+                    multiply_zeros(BRIDGE_PASSES)
+                quantise_slab(2 * i)
+            if 0 <= c < W4_LOADS:
+                negative_branch(c)
+                if c % HALVES == HALVES - 1:
+                    finish_elu(c // HALVES)
 
         out_sum = out_banks.tile([P, PIXELS], F32)
-        for g in range(GROUPS):
-            s = W4_LOADS * PAIR + g
-            for second_pass in range(PASSES):
+        for second_pass in range(PASSES):
+            for g in range(GROUPS):
+                s = W4_LOADS * PAIR + g
                 nc.tensor.matmul_mx(
                     out=out_sum[:],
                     lhsT=codes[s][:, second_pass, :].bitcast(FP8X4),
                     lhsT_scale=scales[s][:, second_pass, :],
                     rhs=h4_codes[:, second_pass, :].bitcast(FP8X4),
                     rhs_scale=h4_scales[:, second_pass, :],
-                    start=(g == 0 and second_pass == 0),
-                    stop=(g == GROUPS - 1 and second_pass == PASSES - 1),
+                    start=(second_pass == 0 and g == 0),
+                    stop=(second_pass == PASSES - 1 and g == GROUPS - 1),
                 )
 
         result = keep.tile([P, PIXELS], F32)

@@ -31,6 +31,7 @@ TRANSPOSE_BANKS = 5
 UNREAD_COLUMNS = 256
 WARM_UP_PASSES = 10
 BRIDGE_PASSES = 6
+KEEP_PASSES = 2
 LOAD_LAG = 2
 
 FLOPS = 2 * PIXELS * K * K + 2 * PIXELS * K * PARTS * GROUPS * D
@@ -84,11 +85,14 @@ def tile_qca_operator_deep_pb_s_kernel(tc, h3, w4, w5, out):
         nc.vector.memset(zeros[:].bitcast(I32), 0)
         nc.vector.quantize_mx(out=zero_codes[:].bitcast(FP8X4), scales=zero_scales[:], in_=zeros[:])
 
+        out_bank = out_banks.tile([P, 2 * UNREAD_COLUMNS], F32)
+        out_sum = out_bank[:, 0:PIXELS]
+        unread = out_bank[:, UNREAD_COLUMNS : 2 * UNREAD_COLUMNS]
+
         def multiply_zeros(passes):
-            unread = banks.tile([P, UNREAD_COLUMNS], F32, tag="bank")
             for i in range(passes):
                 nc.tensor.matmul_mx(
-                    out=unread[:],
+                    out=unread,
                     lhsT=zero_codes[:, 0:P].bitcast(FP8X4),
                     lhsT_scale=zero_scales[:, 0:P],
                     rhs=zero_codes[:].bitcast(FP8X4),
@@ -192,6 +196,8 @@ def tile_qca_operator_deep_pb_s_kernel(tc, h3, w4, w5, out):
                 quantise_slab(2 * i - 1)
                 if c >= 1 and (c - 1) % HALVES == HALVES - 1:
                     quantise_h4((c - 1) // HALVES)
+            if 1 <= i < SLAB_PAIRS:
+                multiply_zeros(KEEP_PASSES)
             if 0 <= c < W4_LOADS:
                 first_layer_and_exp(c)
             if i < SLAB_PAIRS:
@@ -204,12 +210,11 @@ def tile_qca_operator_deep_pb_s_kernel(tc, h3, w4, w5, out):
                 if c % HALVES == HALVES - 1:
                     finish_elu(c // HALVES)
 
-        out_sum = out_banks.tile([P, PIXELS], F32)
         for second_pass in range(PASSES):
             for g in range(GROUPS):
                 s = W4_LOADS * PAIR + g
                 nc.tensor.matmul_mx(
-                    out=out_sum[:],
+                    out=out_sum,
                     lhsT=codes[s][:, second_pass, :].bitcast(FP8X4),
                     lhsT_scale=scales[s][:, second_pass, :],
                     rhs=h4_codes[:, second_pass, :].bitcast(FP8X4),
@@ -219,7 +224,7 @@ def tile_qca_operator_deep_pb_s_kernel(tc, h3, w4, w5, out):
                 )
 
         result = keep.tile([P, PIXELS], F32)
-        nc.vector.tensor_scalar_mul(out=result[:], in0=out_sum[:], scalar1=0.1 / GROUPS)
+        nc.vector.tensor_scalar_mul(out=result[:], in0=out_sum, scalar1=0.1 / GROUPS)
         for h in range(PARTS):
             nc.sync.dma_start(
                 out=out[:, h * D : (h + 1) * D].rearrange("b d i j -> d b (i j)"),

@@ -29,10 +29,11 @@ SLABS = W4_LOADS * PAIR + GROUPS
 SLAB_PAIRS = SLABS // 2
 TRANSPOSE_BANKS = 5
 UNREAD_COLUMNS = 256
-WARM_UP_PASSES = 10
-BRIDGE_PASSES = 6
+WARM_UP_PASSES = 5
+BRIDGE_PASSES = 5
 KEEP_PASSES = 2
-LOAD_LAG = 2
+PRODUCT_LAG = 4
+VECTOR_COPIES = (3, 7)
 
 FLOPS = 2 * PIXELS * K * K + 2 * PIXELS * K * PARTS * GROUPS * D
 
@@ -46,25 +47,29 @@ def tile_qca_operator_deep_pb_s_kernel(tc, h3, w4, w5, out):
         out_banks = ctx.enter_context(tc.psum_pool(name="out_banks", bufs=1))
         ctx.enter_context(tc.manual_schedule())
 
-        w4_raw = [keep.tile([P, PAIR, K], BF16, name="w4_raw%d" % c) for c in range(W4_LOADS)]
-        w4_rows = w4.rearrange("(c p e) k -> c p e k", p=P, e=PAIR)
+        w4_raw = [keep.tile([P, K], BF16, name="w4_raw%d" % s) for s in range(W4_LOADS * PAIR)]
+        w4_rows = w4.rearrange("(c p e) k -> c e p k", p=P, e=PAIR)
         h3_raw = keep.tile([P, BATCH, PASSES * PACK, PIXELS_PER_IMAGE], BF16)
         w5_raw = [keep.tile([P, K], BF16, name="w5_raw%d" % g) for g in range(GROUPS)]
 
-        nc.sync.dma_start(out=w4_raw[0][:], in_=w4_rows[0])
+        def load_w4(s):
+            nc.sync.dma_start(out=w4_raw[s][:], in_=w4_rows[s // PAIR, s % PAIR])
+
+        for s in range(PAIR):
+            load_w4(s)
         for b in range(BATCH):
             nc.sync.dma_start(
                 out=h3_raw[:, b].rearrange("q (c e) x -> q c (e x)", e=PAIR),
                 in_=h3[b].rearrange("(c q e) i j -> q c (e i j)", q=P, e=PAIR),
             )
-        for c in range(1, W4_LOADS):
-            nc.sync.dma_start(out=w4_raw[c][:], in_=w4_rows[c])
+        for s in range(PAIR, W4_LOADS * PAIR):
+            load_w4(s)
         for g in range(GROUPS):
             for h in range(PARTS):
                 first_row = (h * GROUPS + g) * D
                 nc.sync.dma_start(out=w5_raw[g][h:P:PARTS, :], in_=w5[first_row : first_row + D, :])
 
-        slab_words = [w4_raw[c][:].bitcast(F32)[:, e, :] for c in range(W4_LOADS) for e in range(PAIR)]
+        slab_words = [w4_raw[s][:].bitcast(F32) for s in range(W4_LOADS * PAIR)]
         slab_words.extend([w5_raw[g][:].bitcast(F32) for g in range(GROUPS)])
         grouped = [
             keep.tile([P, PASSES, P, PACK], BF16, name="grouped%d" % s, align_bytes=64) for s in range(SLABS)
@@ -106,16 +111,18 @@ def tile_qca_operator_deep_pb_s_kernel(tc, h3, w4, w5, out):
         h3_grouped = keep.tile([P, PASSES, PIXELS, PACK], BF16, align_bytes=64)
         h3_codes = keep.tile([P, PASSES, PIXELS], U32, align_bytes=64)
         h3_scales = keep.tile([P, PASSES, PIXELS], U8, align_bytes=64)
-        for a in range(PASSES):
+        def group_h3(a):
             nc.vector.tensor_copy(
                 out=h3_grouped[:, a].rearrange("q (b x) t -> q b x t", b=BATCH),
                 in_=h3_raw[:, :, a * PACK : (a + 1) * PACK, :].rearrange("q b t x -> q b x t"),
             )
-        nc.vector.quantize_mx(
-            out=h3_codes[:].rearrange("q a n -> q (a n)").bitcast(FP8X4),
-            scales=h3_scales[:].rearrange("q a n -> q (a n)"),
-            in_=h3_grouped[:].rearrange("q a n t -> q (a n t)"),
-        )
+
+        def quantise_h3():
+            nc.vector.quantize_mx(
+                out=h3_codes[:].rearrange("q a n -> q (a n)").bitcast(FP8X4),
+                scales=h3_scales[:].rearrange("q a n -> q (a n)"),
+                in_=h3_grouped[:].rearrange("q a n t -> q (a n t)"),
+            )
 
         h4_sum = [h4_banks.tile([P, PACK, PIXELS], F32, name="h4_sum%d" % a) for a in range(PASSES)]
         exp_v = [keep.tile([P, PACK, PIXELS], F32, name="exp_v%d" % a) for a in range(PASSES)]
@@ -134,7 +141,8 @@ def tile_qca_operator_deep_pb_s_kernel(tc, h3, w4, w5, out):
                     nc.tensor.transpose(
                         bank[:, a, u, :], slab_words[s][:, first_word : first_word + P], identity[:]
                     )
-            nc.scalar.copy(out=grouped[s][:].bitcast(F32), in_=bank[:].rearrange("q a u r -> q a r u"))
+            copy = nc.vector.tensor_copy if s in VECTOR_COPIES else nc.scalar.copy
+            copy(out=grouped[s][:].bitcast(F32), in_=bank[:].rearrange("q a u r -> q a r u"))
 
         def quantise_slab(s):
             nc.vector.quantize_mx(
@@ -188,27 +196,29 @@ def tile_qca_operator_deep_pb_s_kernel(tc, h3, w4, w5, out):
                 in_=h4_grouped[second_pass][:].rearrange("p n t -> p (n t)"),
             )
 
-        for i in range(SLAB_PAIRS + 1):
-            c = i - LOAD_LAG
-            if i < SLAB_PAIRS:
-                transpose_and_copy(2 * i)
-            if i >= 1:
-                quantise_slab(2 * i - 1)
-                if c >= 1 and (c - 1) % HALVES == HALVES - 1:
-                    quantise_h4((c - 1) // HALVES)
-            if 1 <= i < SLAB_PAIRS:
-                multiply_zeros(KEEP_PASSES)
-            if 0 <= c < W4_LOADS:
-                first_layer_and_exp(c)
-            if i < SLAB_PAIRS:
-                transpose_and_copy(2 * i + 1)
-                if i == 0:
-                    multiply_zeros(BRIDGE_PASSES)
-                quantise_slab(2 * i)
-            if 0 <= c < W4_LOADS:
-                negative_branch(c)
-                if c % HALVES == HALVES - 1:
-                    finish_elu(c // HALVES)
+        for s in range(SLABS + 2):
+            if s < SLABS:
+                transpose_and_copy(s)
+            if s == 1:
+                multiply_zeros(BRIDGE_PASSES)
+                for a in range(PASSES):
+                    group_h3(a)
+            if 1 <= s <= SLABS:
+                quantise_slab(s - 1)
+            if s == 1:
+                quantise_h3()
+            for c in range(W4_LOADS):
+                if s == PAIR * c + PRODUCT_LAG:
+                    multiply_zeros(KEEP_PASSES)
+                    first_layer_and_exp(c)
+                if s == PAIR * c + PRODUCT_LAG + 1:
+                    negative_branch(c)
+            for second_pass in range(PASSES):
+                due = (second_pass + 1) * PASSES * PAIR + PRODUCT_LAG
+                if s == due:
+                    finish_elu(second_pass)
+                if s == due + 1:
+                    quantise_h4(second_pass)
 
         for second_pass in range(PASSES):
             for g in range(GROUPS):

@@ -25,8 +25,9 @@ W4_LOADS = 4
 GROUPS = 4
 PARTS = 2
 D = 64
-SLABS = W4_LOADS * PAIR + GROUPS
-SLAB_PAIRS = SLABS // 2
+W4_SLABS = W4_LOADS * PAIR
+W5_PAIRS = GROUPS // PAIR
+SLABS = W4_SLABS + W5_PAIRS * PARTS
 TRANSPOSE_BANKS = 5
 UNREAD_COLUMNS = 256
 WARM_UP_PASSES = 5
@@ -47,35 +48,38 @@ def tile_qca_operator_deep_pb_s_kernel(tc, h3, w4, w5, out):
         out_banks = ctx.enter_context(tc.psum_pool(name="out_banks", bufs=1))
         ctx.enter_context(tc.manual_schedule())
 
-        w4_raw = [keep.tile([P, K], BF16, name="w4_raw%d" % s) for s in range(W4_LOADS * PAIR)]
-        w4_rows = w4.rearrange("(c p e) k -> c e p k", p=P, e=PAIR)
+        w4_raw = [keep.tile([P, PAIR, K], BF16, name="w4_raw%d" % c) for c in range(W4_LOADS)]
+        w4_rows = w4.rearrange("(c p e) k -> c p e k", p=P, e=PAIR)
         h3_raw = keep.tile([P, BATCH, PASSES * PACK, PIXELS_PER_IMAGE], BF16)
-        w5_raw = [keep.tile([P, K], BF16, name="w5_raw%d" % g) for g in range(GROUPS)]
+        w5_raw = [keep.tile([P, K], BF16, name="w5_raw%d" % i) for i in range(W5_PAIRS * PARTS)]
 
-        def load_w4(s):
-            nc.sync.dma_start(out=w4_raw[s][:], in_=w4_rows[s // PAIR, s % PAIR])
-
-        for s in range(PAIR):
-            load_w4(s)
+        for e in range(PAIR):
+            nc.sync.dma_start(out=w4_raw[0][:, e, :], in_=w4_rows[0, :, e, :])
         for b in range(BATCH):
             nc.sync.dma_start(
                 out=h3_raw[:, b].rearrange("q (c e) x -> q c (e x)", e=PAIR),
                 in_=h3[b].rearrange("(c q e) i j -> q c (e i j)", q=P, e=PAIR),
             )
-        for s in range(PAIR, W4_LOADS * PAIR):
-            load_w4(s)
-        for g in range(GROUPS):
+        for c in range(1, W4_LOADS):
+            nc.sync.dma_start(out=w4_raw[c][:], in_=w4_rows[c])
+        for v in range(W5_PAIRS):
             for h in range(PARTS):
-                first_row = (h * GROUPS + g) * D
-                nc.sync.dma_start(out=w5_raw[g][h:P:PARTS, :], in_=w5[first_row : first_row + D, :])
+                first_row = (h * W5_PAIRS + v) * P
+                nc.sync.dma_start(out=w5_raw[v * PARTS + h][:], in_=w5[first_row : first_row + P, :])
 
-        slab_words = [w4_raw[s][:].bitcast(F32) for s in range(W4_LOADS * PAIR)]
-        slab_words.extend([w5_raw[g][:].bitcast(F32) for g in range(GROUPS)])
+        slab_words = [w4_raw[c][:].bitcast(F32)[:, e, :] for c in range(W4_LOADS) for e in range(PAIR)]
+        slab_words.extend([raw[:].bitcast(F32) for raw in w5_raw])
         grouped = [
-            keep.tile([P, PASSES, P, PACK], BF16, name="grouped%d" % s, align_bytes=64) for s in range(SLABS)
+            keep.tile([P, PASSES, P, PACK], BF16, name="grouped%d" % s, align_bytes=64) for s in range(W4_SLABS)
         ]
-        codes = [keep.tile([P, PASSES, P], U32, name="codes%d" % s, align_bytes=64) for s in range(SLABS)]
-        scales = [keep.tile([P, PASSES, P], U8, name="scales%d" % s, align_bytes=64) for s in range(SLABS)]
+        codes = [keep.tile([P, PASSES, P], U32, name="codes%d" % s, align_bytes=64) for s in range(W4_SLABS)]
+        scales = [keep.tile([P, PASSES, P], U8, name="scales%d" % s, align_bytes=64) for s in range(W4_SLABS)]
+        w5_grouped = [
+            keep.tile([P, PASSES, PAIR, PARTS, D, PACK], BF16, name="w5_grouped%d" % v, align_bytes=64)
+            for v in range(W5_PAIRS)
+        ]
+        w5_codes = [keep.tile([P, PASSES, PAIR, P], U32, name="w5_codes%d" % v, align_bytes=64) for v in range(W5_PAIRS)]
+        w5_scales = [keep.tile([P, PASSES, PAIR, P], U8, name="w5_scales%d" % v, align_bytes=64) for v in range(W5_PAIRS)]
 
         identity = keep.tile([P, P], F32)
         make_identity(nc, identity[:])
@@ -134,21 +138,35 @@ def tile_qca_operator_deep_pb_s_kernel(tc, h3, w4, w5, out):
         h4_scales = keep.tile([P, PASSES, PIXELS], U8, align_bytes=64)
 
         def transpose_and_copy(s):
-            bank = banks.tile([P, PASSES, HALVES, P], F32)
+            bank = banks.tile([P, HALVES, PASSES, P], F32)
             for a in range(PASSES):
                 for u in range(HALVES):
                     first_word = (a * HALVES + u) * P
                     nc.tensor.transpose(
-                        bank[:, a, u, :], slab_words[s][:, first_word : first_word + P], identity[:]
+                        bank[:, u, a, :], slab_words[s][:, first_word : first_word + P], identity[:]
                     )
             copy = nc.vector.tensor_copy if s in VECTOR_COPIES else nc.scalar.copy
-            copy(out=grouped[s][:].bitcast(F32), in_=bank[:].rearrange("q a u r -> q a r u"))
+            if s < W4_SLABS:
+                copy(out=grouped[s][:].bitcast(F32), in_=bank[:].rearrange("q u a r -> q a r u"))
+            else:
+                v, h = divmod(s - W4_SLABS, PARTS)
+                copy(
+                    out=w5_grouped[v][:, :, :, h].bitcast(F32).rearrange("q a i d u -> q (a i) d u"),
+                    in_=bank[:].rearrange("q u a (i d) -> q (a i) d u", i=PAIR),
+                )
 
         def quantise_slab(s):
             nc.vector.quantize_mx(
                 out=codes[s][:].rearrange("q a r -> q (a r)").bitcast(FP8X4),
                 scales=scales[s][:].rearrange("q a r -> q (a r)"),
                 in_=grouped[s][:].rearrange("q a r t -> q (a r t)"),
+            )
+
+        def quantise_w5(v, a):
+            nc.vector.quantize_mx(
+                out=w5_codes[v][:, a].rearrange("q i m -> q (i m)").bitcast(FP8X4),
+                scales=w5_scales[v][:, a].rearrange("q i m -> q (i m)"),
+                in_=w5_grouped[v][:, a].rearrange("q i h d t -> q (i h d t)"),
             )
 
         def first_layer_and_exp(c):
@@ -203,8 +221,12 @@ def tile_qca_operator_deep_pb_s_kernel(tc, h3, w4, w5, out):
                 multiply_zeros(BRIDGE_PASSES)
                 for a in range(PASSES):
                     group_h3(a)
-            if 1 <= s <= SLABS:
+            if 1 <= s <= W4_SLABS:
                 quantise_slab(s - 1)
+            for v in range(W5_PAIRS):
+                for a in range(PASSES):
+                    if s == W4_SLABS + PARTS * (v + 1) + a:
+                        quantise_w5(v, a)
             if s == 1:
                 quantise_h3()
             for c in range(W4_LOADS):
@@ -222,11 +244,11 @@ def tile_qca_operator_deep_pb_s_kernel(tc, h3, w4, w5, out):
 
         for second_pass in range(PASSES):
             for g in range(GROUPS):
-                s = W4_LOADS * PAIR + g
+                v, i = divmod(g, PAIR)
                 nc.tensor.matmul_mx(
                     out=out_sum,
-                    lhsT=codes[s][:, second_pass, :].bitcast(FP8X4),
-                    lhsT_scale=scales[s][:, second_pass, :],
+                    lhsT=w5_codes[v][:, second_pass, i, :].bitcast(FP8X4),
+                    lhsT_scale=w5_scales[v][:, second_pass, i, :],
                     rhs=h4_codes[:, second_pass, :].bitcast(FP8X4),
                     rhs_scale=h4_scales[:, second_pass, :],
                     start=(second_pass == 0 and g == 0),
@@ -235,8 +257,6 @@ def tile_qca_operator_deep_pb_s_kernel(tc, h3, w4, w5, out):
 
         result = keep.tile([P, PIXELS], F32)
         nc.vector.tensor_scalar_mul(out=result[:], in0=out_sum, scalar1=0.1 / GROUPS)
-        for h in range(PARTS):
-            nc.sync.dma_start(
-                out=out[:, h * D : (h + 1) * D].rearrange("b d i j -> d b (i j)"),
-                in_=result[h:P:PARTS, :].rearrange("m (b x) -> m b x", b=BATCH),
-            )
+        nc.sync.dma_start(
+            out=out.rearrange("b m i j -> m b (i j)"), in_=result[:].rearrange("m (b x) -> m b x", b=BATCH)
+        )

@@ -31,9 +31,9 @@ SLABS = W4_SLABS + W5_PAIRS * PARTS
 TRANSPOSE_BANKS = 5
 UNREAD_COLUMNS = 256
 WARM_UP_PASSES = 5
-BRIDGE_PASSES = 5
+BRIDGE_PASSES = 4
 KEEP_PASSES = 2
-PRODUCT_LAG = 4
+PRODUCT_LAG = 3
 VECTOR_COPIES = (3, 7)
 
 FLOPS = 2 * PIXELS * K * K + 2 * PIXELS * K * PARTS * GROUPS * D
@@ -137,23 +137,29 @@ def tile_qca_operator_deep_pb_s_kernel(tc, h3, w4, w5, out):
         h4_codes = keep.tile([P, PASSES, PIXELS], U32, align_bytes=64)
         h4_scales = keep.tile([P, PASSES, PIXELS], U8, align_bytes=64)
 
-        def transpose_and_copy(s):
-            bank = banks.tile([P, HALVES, PASSES, P], F32)
-            for a in range(PASSES):
-                for u in range(HALVES):
-                    first_word = (a * HALVES + u) * P
-                    nc.tensor.transpose(
-                        bank[:, u, a, :], slab_words[s][:, first_word : first_word + P], identity[:]
-                    )
-            copy = nc.vector.tensor_copy if s in VECTOR_COPIES else nc.scalar.copy
+        def transpose_half(bank, s, a):
+            for u in range(HALVES):
+                first_word = (a * HALVES + u) * P
+                nc.tensor.transpose(bank[:, u, a, :], slab_words[s][:, first_word : first_word + P], identity[:])
+
+        def copy_out(copy, s, bank, passes):
             if s < W4_SLABS:
-                copy(out=grouped[s][:].bitcast(F32), in_=bank[:].rearrange("q u a r -> q a r u"))
+                copy(
+                    out=grouped[s][:, passes].bitcast(F32),
+                    in_=bank[:, :, passes, :].rearrange("q u a r -> q a r u"),
+                )
             else:
                 v, h = divmod(s - W4_SLABS, PARTS)
                 copy(
-                    out=w5_grouped[v][:, :, :, h].bitcast(F32).rearrange("q a i d u -> q (a i) d u"),
-                    in_=bank[:].rearrange("q u a (i d) -> q (a i) d u", i=PAIR),
+                    out=w5_grouped[v][:, passes, :, h].bitcast(F32).rearrange("q a i d u -> q (a i) d u"),
+                    in_=bank[:, :, passes, :].rearrange("q u a (i d) -> q (a i) d u", i=PAIR),
                 )
+
+        def transpose_and_copy(s):
+            bank = banks.tile([P, HALVES, PASSES, P], F32, tag="bank")
+            for a in range(PASSES):
+                transpose_half(bank, s, a)
+            copy_out(nc.vector.tensor_copy if s in VECTOR_COPIES else nc.scalar.copy, s, bank, slice(0, PASSES))
 
         def quantise_slab(s):
             nc.vector.quantize_mx(
@@ -214,46 +220,57 @@ def tile_qca_operator_deep_pb_s_kernel(tc, h3, w4, w5, out):
                 in_=h4_grouped[second_pass][:].rearrange("p n t -> p (n t)"),
             )
 
-        for s in range(SLABS + 2):
-            if s < SLABS:
-                transpose_and_copy(s)
+        out_sum_first, out_sum_last = (0, 0), (W5_PAIRS - 1, PASSES - 1)
+
+        def second_layer(v, a):
+            for i in range(PAIR):
+                nc.tensor.matmul_mx(
+                    out=out_sum,
+                    lhsT=w5_codes[v][:, a, i, :].bitcast(FP8X4),
+                    lhsT_scale=w5_scales[v][:, a, i, :],
+                    rhs=h4_codes[:, a, :].bitcast(FP8X4),
+                    rhs_scale=h4_scales[:, a, :],
+                    start=((v, a) == out_sum_first and i == 0),
+                    stop=((v, a) == out_sum_last and i == PAIR - 1),
+                )
+
+        last = SLABS - 1
+        for s in range(last):
+            transpose_and_copy(s)
             if s == 1:
                 multiply_zeros(BRIDGE_PASSES)
                 for a in range(PASSES):
                     group_h3(a)
             if 1 <= s <= W4_SLABS:
                 quantise_slab(s - 1)
-            for v in range(W5_PAIRS):
-                for a in range(PASSES):
-                    if s == W4_SLABS + PARTS * (v + 1) + a:
-                        quantise_w5(v, a)
             if s == 1:
                 quantise_h3()
+            if s == W4_SLABS + PARTS:
+                for a in range(PASSES):
+                    quantise_w5(0, a)
             for c in range(W4_LOADS):
                 if s == PAIR * c + PRODUCT_LAG:
                     multiply_zeros(KEEP_PASSES)
                     first_layer_and_exp(c)
                 if s == PAIR * c + PRODUCT_LAG + 1:
                     negative_branch(c)
-            for second_pass in range(PASSES):
-                due = (second_pass + 1) * PASSES * PAIR + PRODUCT_LAG
-                if s == due:
-                    finish_elu(second_pass)
-                if s == due + 1:
-                    quantise_h4(second_pass)
+            if s == W4_SLABS:
+                finish_elu(0)
+            if s == W4_SLABS + 1:
+                quantise_h4(0)
 
-        for second_pass in range(PASSES):
-            for g in range(GROUPS):
-                v, i = divmod(g, PAIR)
-                nc.tensor.matmul_mx(
-                    out=out_sum,
-                    lhsT=w5_codes[v][:, second_pass, i, :].bitcast(FP8X4),
-                    lhsT_scale=w5_scales[v][:, second_pass, i, :],
-                    rhs=h4_codes[:, second_pass, :].bitcast(FP8X4),
-                    rhs_scale=h4_scales[:, second_pass, :],
-                    start=(second_pass == 0 and g == 0),
-                    stop=(second_pass == PASSES - 1 and g == GROUPS - 1),
-                )
+        half_banks = [banks.tile([P, HALVES, PASSES, P], F32, tag="bank", name="half_bank%d" % a) for a in range(PASSES)]
+        for a in range(PASSES):
+            transpose_half(half_banks[a], last, a)
+        copy_out(nc.scalar.copy, last, half_banks[0], slice(0, 1))
+        finish_elu(1)
+        copy_out(nc.vector.tensor_copy, last, half_banks[1], slice(1, 2))
+        quantise_h4(1)
+        for v in range(W5_PAIRS):
+            for a in range(PASSES):
+                if v == W5_PAIRS - 1:
+                    quantise_w5(v, a)
+                second_layer(v, a)
 
         result = keep.tile([P, PIXELS], F32)
         nc.vector.tensor_scalar_mul(out=result[:], in0=out_sum, scalar1=0.1 / GROUPS)

@@ -29,12 +29,12 @@ W4_SLABS = W4_LOADS * PAIR
 W5_PAIRS = GROUPS // PAIR
 SLABS = W4_SLABS + W5_PAIRS * PARTS
 TRANSPOSE_BANKS = 5
-UNREAD_COLUMNS = 256
-WARM_UP_PASSES = 5
-BRIDGE_PASSES = 4
-KEEP_PASSES = 2
+UNREAD_COLUMNS = 128
+WARM_UP_PASSES = 14
+BRIDGE_PASSES = 12
+TAIL_PASSES = 3
+KEEP_PASSES = 4
 PRODUCT_LAG = 3
-VECTOR_COPIES = (3, 7)
 
 FLOPS = 2 * PIXELS * K * K + 2 * PIXELS * K * PARTS * GROUPS * D
 
@@ -84,14 +84,14 @@ def tile_qca_operator_deep_pb_s_kernel(tc, h3, w4, w5, out):
         identity = keep.tile([P, P], F32)
         make_identity(nc, identity[:])
 
-        table_warmer = keep.tile([P, 1], F32)
-        nc.vector.memset(table_warmer[:], 0.0)
-        nc.scalar.activation(out=table_warmer[:], in_=table_warmer[:], func=ACT.Exp)
 
         zeros = keep.tile([P, UNREAD_COLUMNS * PACK], BF16, align_bytes=64)
         zero_codes = keep.tile([P, UNREAD_COLUMNS], U32, align_bytes=64)
         zero_scales = keep.tile([P, UNREAD_COLUMNS], U8, align_bytes=64)
         nc.vector.memset(zeros[:].bitcast(I32), 0)
+        table_warmer = keep.tile([P, 1], F32)
+        nc.vector.memset(table_warmer[:], 0.0)
+        nc.scalar.activation(out=table_warmer[:], in_=table_warmer[:], func=ACT.Exp)
         nc.vector.quantize_mx(out=zero_codes[:].bitcast(FP8X4), scales=zero_scales[:], in_=zeros[:])
 
         out_bank = out_banks.tile([P, 2 * UNREAD_COLUMNS], F32)
@@ -142,15 +142,15 @@ def tile_qca_operator_deep_pb_s_kernel(tc, h3, w4, w5, out):
                 first_word = (a * HALVES + u) * P
                 nc.tensor.transpose(bank[:, u, a, :], slab_words[s][:, first_word : first_word + P], identity[:])
 
-        def copy_out(copy, s, bank, passes):
+        def copy_out(s, bank, passes):
             if s < W4_SLABS:
-                copy(
+                nc.scalar.copy(
                     out=grouped[s][:, passes].bitcast(F32),
                     in_=bank[:, :, passes, :].rearrange("q u a r -> q a r u"),
                 )
             else:
                 v, h = divmod(s - W4_SLABS, PARTS)
-                copy(
+                nc.scalar.copy(
                     out=w5_grouped[v][:, passes, :, h].bitcast(F32).rearrange("q a i d u -> q (a i) d u"),
                     in_=bank[:, :, passes, :].rearrange("q u a (i d) -> q (a i) d u", i=PAIR),
                 )
@@ -159,7 +159,7 @@ def tile_qca_operator_deep_pb_s_kernel(tc, h3, w4, w5, out):
             bank = banks.tile([P, HALVES, PASSES, P], F32, tag="bank")
             for a in range(PASSES):
                 transpose_half(bank, s, a)
-            copy_out(nc.vector.tensor_copy if s in VECTOR_COPIES else nc.scalar.copy, s, bank, slice(0, PASSES))
+            copy_out(s, bank, slice(0, PASSES))
 
         def quantise_slab(s):
             nc.vector.quantize_mx(
@@ -236,6 +236,8 @@ def tile_qca_operator_deep_pb_s_kernel(tc, h3, w4, w5, out):
 
         last = SLABS - 1
         for s in range(last):
+            if s == last - 1:
+                multiply_zeros(TAIL_PASSES)
             transpose_and_copy(s)
             if s == 1:
                 multiply_zeros(BRIDGE_PASSES)
@@ -259,12 +261,14 @@ def tile_qca_operator_deep_pb_s_kernel(tc, h3, w4, w5, out):
             if s == W4_SLABS + 1:
                 quantise_h4(0)
 
+        multiply_zeros(TAIL_PASSES)
         half_banks = [banks.tile([P, HALVES, PASSES, P], F32, tag="bank", name="half_bank%d" % a) for a in range(PASSES)]
         for a in range(PASSES):
             transpose_half(half_banks[a], last, a)
-        copy_out(nc.scalar.copy, last, half_banks[0], slice(0, 1))
+        for a in range(PASSES):
+            copy_out(last, half_banks[a], slice(a, a + 1))
         finish_elu(1)
-        copy_out(nc.vector.tensor_copy, last, half_banks[1], slice(1, 2))
+        multiply_zeros(TAIL_PASSES)
         quantise_h4(1)
         for v in range(W5_PAIRS):
             for a in range(PASSES):

@@ -32,7 +32,9 @@ TRANSPOSE_BANKS = 5
 UNREAD_COLUMNS = 128
 WARM_UP_PASSES = 14
 BRIDGE_PASSES = 12
-TAIL_PASSES = 3
+VECTOR_COPIES = (3,)
+LAST_PASSES = 6
+TAIL_PASSES = 4
 KEEP_PASSES = 4
 PRODUCT_LAG = 3
 
@@ -51,10 +53,10 @@ def tile_qca_operator_deep_pb_s_kernel(tc, h3, w4, w5, out):
         w4_raw = [keep.tile([P, PAIR, K], BF16, name="w4_raw%d" % c) for c in range(W4_LOADS)]
         w4_rows = w4.rearrange("(c p e) k -> c p e k", p=P, e=PAIR)
         h3_raw = keep.tile([P, BATCH, PASSES * PACK, PIXELS_PER_IMAGE], BF16)
-        w5_raw = [keep.tile([P, K], BF16, name="w5_raw%d" % i) for i in range(W5_PAIRS * PARTS)]
+        w5_raw = [keep.tile([P, W5_PAIRS, K], BF16, name="w5_raw%d" % h) for h in range(PARTS)]
+        w5_rows = w5.rearrange("(h v p) k -> h p v k", h=PARTS, p=P)
 
-        for e in range(PAIR):
-            nc.sync.dma_start(out=w4_raw[0][:, e, :], in_=w4_rows[0, :, e, :])
+        nc.sync.dma_start(out=w4_raw[0][:], in_=w4_rows[0])
         for b in range(BATCH):
             nc.sync.dma_start(
                 out=h3_raw[:, b].rearrange("q (c e) x -> q c (e x)", e=PAIR),
@@ -62,13 +64,12 @@ def tile_qca_operator_deep_pb_s_kernel(tc, h3, w4, w5, out):
             )
         for c in range(1, W4_LOADS):
             nc.sync.dma_start(out=w4_raw[c][:], in_=w4_rows[c])
+        nc.sync.dma_start(out=w5_raw[0][:], in_=w5_rows[0])
         for v in range(W5_PAIRS):
-            for h in range(PARTS):
-                first_row = (h * W5_PAIRS + v) * P
-                nc.sync.dma_start(out=w5_raw[v * PARTS + h][:], in_=w5[first_row : first_row + P, :])
+            nc.sync.dma_start(out=w5_raw[1][:, v, :], in_=w5_rows[1, :, v, :])
 
         slab_words = [w4_raw[c][:].bitcast(F32)[:, e, :] for c in range(W4_LOADS) for e in range(PAIR)]
-        slab_words.extend([raw[:].bitcast(F32) for raw in w5_raw])
+        slab_words.extend([w5_raw[h][:].bitcast(F32)[:, v, :] for v in range(W5_PAIRS) for h in range(PARTS)])
         grouped = [
             keep.tile([P, PASSES, P, PACK], BF16, name="grouped%d" % s, align_bytes=64) for s in range(W4_SLABS)
         ]
@@ -142,15 +143,15 @@ def tile_qca_operator_deep_pb_s_kernel(tc, h3, w4, w5, out):
                 first_word = (a * HALVES + u) * P
                 nc.tensor.transpose(bank[:, u, a, :], slab_words[s][:, first_word : first_word + P], identity[:])
 
-        def copy_out(s, bank, passes):
+        def copy_out(copy, s, bank, passes):
             if s < W4_SLABS:
-                nc.scalar.copy(
+                copy(
                     out=grouped[s][:, passes].bitcast(F32),
                     in_=bank[:, :, passes, :].rearrange("q u a r -> q a r u"),
                 )
             else:
                 v, h = divmod(s - W4_SLABS, PARTS)
-                nc.scalar.copy(
+                copy(
                     out=w5_grouped[v][:, passes, :, h].bitcast(F32).rearrange("q a i d u -> q (a i) d u"),
                     in_=bank[:, :, passes, :].rearrange("q u a (i d) -> q (a i) d u", i=PAIR),
                 )
@@ -159,7 +160,7 @@ def tile_qca_operator_deep_pb_s_kernel(tc, h3, w4, w5, out):
             bank = banks.tile([P, HALVES, PASSES, P], F32, tag="bank")
             for a in range(PASSES):
                 transpose_half(bank, s, a)
-            copy_out(s, bank, slice(0, PASSES))
+            copy_out(nc.vector.tensor_copy if s in VECTOR_COPIES else nc.scalar.copy, s, bank, slice(0, PASSES))
 
         def quantise_slab(s):
             nc.vector.quantize_mx(
@@ -262,13 +263,9 @@ def tile_qca_operator_deep_pb_s_kernel(tc, h3, w4, w5, out):
                 quantise_h4(0)
 
         multiply_zeros(TAIL_PASSES)
-        half_banks = [banks.tile([P, HALVES, PASSES, P], F32, tag="bank", name="half_bank%d" % a) for a in range(PASSES)]
-        for a in range(PASSES):
-            transpose_half(half_banks[a], last, a)
-        for a in range(PASSES):
-            copy_out(last, half_banks[a], slice(a, a + 1))
+        transpose_and_copy(last)
         finish_elu(1)
-        multiply_zeros(TAIL_PASSES)
+        multiply_zeros(LAST_PASSES)
         quantise_h4(1)
         for v in range(W5_PAIRS):
             for a in range(PASSES):

@@ -30,12 +30,12 @@ W5_PAIRS = GROUPS // PAIR
 SLABS = W4_SLABS + W5_PAIRS * PARTS
 TRANSPOSE_BANKS = 5
 UNREAD_COLUMNS = 128
-WARM_UP_PASSES = 14
-BRIDGE_PASSES = 12
-VECTOR_COPIES = (3,)
-LAST_PASSES = 6
-TAIL_PASSES = 4
-KEEP_PASSES = 4
+WARM_UP_PASSES = 16
+BRIDGE_PASSES = 8
+VECTOR_COPIES = (3, 5, 7)
+LAST_PASSES = 14
+KEEP_PASSES = 5
+NEGATIVE_LAG = 6
 PRODUCT_LAG = 3
 
 FLOPS = 2 * PIXELS * K * K + 2 * PIXELS * K * PARTS * GROUPS * D
@@ -235,43 +235,38 @@ def tile_qca_operator_deep_pb_s_kernel(tc, h3, w4, w5, out):
                     stop=((v, a) == out_sum_last and i == PAIR - 1),
                 )
 
-        last = SLABS - 1
-        for s in range(last):
-            if s == last - 1:
-                multiply_zeros(TAIL_PASSES)
+        for s in range(SLABS):
             transpose_and_copy(s)
             if s == 1:
                 multiply_zeros(BRIDGE_PASSES)
                 for a in range(PASSES):
                     group_h3(a)
+                quantise_h3()
             if 1 <= s <= W4_SLABS:
                 quantise_slab(s - 1)
-            if s == 1:
-                quantise_h3()
             if s == W4_SLABS + PARTS:
-                for a in range(PASSES):
-                    quantise_w5(0, a)
+                quantise_w5(0, 0)
+                quantise_h4(0)
             for c in range(W4_LOADS):
                 if s == PAIR * c + PRODUCT_LAG:
                     multiply_zeros(KEEP_PASSES)
                     first_layer_and_exp(c)
-                if s == PAIR * c + PRODUCT_LAG + 1:
+                if s == PAIR * (c - c // HALVES) + NEGATIVE_LAG:
                     negative_branch(c)
-            if s == W4_SLABS:
-                finish_elu(0)
             if s == W4_SLABS + 1:
-                quantise_h4(0)
-
-        multiply_zeros(TAIL_PASSES)
-        transpose_and_copy(last)
+                finish_elu(0)
+            if s == W4_SLABS + PARTS:
+                quantise_w5(0, 1)
         finish_elu(1)
+
         multiply_zeros(LAST_PASSES)
+        second_layer(0, 0)
+        quantise_w5(1, 0)
         quantise_h4(1)
-        for v in range(W5_PAIRS):
-            for a in range(PASSES):
-                if v == W5_PAIRS - 1:
-                    quantise_w5(v, a)
-                second_layer(v, a)
+        second_layer(0, 1)
+        second_layer(1, 0)
+        quantise_w5(1, 1)
+        second_layer(1, 1)
 
         result = keep.tile([P, PIXELS], F32)
         nc.vector.tensor_scalar_mul(out=result[:], in0=out_sum, scalar1=0.1 / GROUPS)

@@ -32,10 +32,10 @@ TRANSPOSE_BANKS = 5
 UNREAD_COLUMNS = 128
 WARM_UP_PASSES = 16
 BRIDGE_PASSES = 8
-VECTOR_COPIES = (3, 5, 7)
+SHARED_SLABS = (3, 5, 7)
 LAST_PASSES = 14
-KEEP_PASSES = 5
-NEGATIVE_LAG = 6
+KEEP_PASSES = 4
+NEGATIVE_LAG = 4
 PRODUCT_LAG = 3
 
 FLOPS = 2 * PIXELS * K * K + 2 * PIXELS * K * PARTS * GROUPS * D
@@ -116,10 +116,10 @@ def tile_qca_operator_deep_pb_s_kernel(tc, h3, w4, w5, out):
         h3_grouped = keep.tile([P, PASSES, PIXELS, PACK], BF16, align_bytes=64)
         h3_codes = keep.tile([P, PASSES, PIXELS], U32, align_bytes=64)
         h3_scales = keep.tile([P, PASSES, PIXELS], U8, align_bytes=64)
-        def group_h3(a):
+        def group_h3(b):
+            pixels = slice(b * PIXELS_PER_IMAGE, (b + 1) * PIXELS_PER_IMAGE)
             nc.vector.tensor_copy(
-                out=h3_grouped[:, a].rearrange("q (b x) t -> q b x t", b=BATCH),
-                in_=h3_raw[:, :, a * PACK : (a + 1) * PACK, :].rearrange("q b t x -> q b x t"),
+                out=h3_grouped[:, :, pixels, :], in_=h3_raw[:, b].rearrange("q (a t) x -> q a x t", t=PACK)
             )
 
         def quantise_h3():
@@ -157,10 +157,16 @@ def tile_qca_operator_deep_pb_s_kernel(tc, h3, w4, w5, out):
                 )
 
         def transpose_and_copy(s):
-            bank = banks.tile([P, HALVES, PASSES, P], F32, tag="bank")
-            for a in range(PASSES):
-                transpose_half(bank, s, a)
-            copy_out(nc.vector.tensor_copy if s in VECTOR_COPIES else nc.scalar.copy, s, bank, slice(0, PASSES))
+            if s in SHARED_SLABS:
+                for a, copy in enumerate((nc.scalar.copy, nc.vector.tensor_copy)):
+                    bank = banks.tile([P, HALVES, PASSES, P], F32, tag="bank", name="half%d" % a)
+                    transpose_half(bank, s, a)
+                    copy_out(copy, s, bank, slice(a, a + 1))
+            else:
+                bank = banks.tile([P, HALVES, PASSES, P], F32, tag="bank")
+                for a in range(PASSES):
+                    transpose_half(bank, s, a)
+                copy_out(nc.scalar.copy, s, bank, slice(0, PASSES))
 
         def quantise_slab(s):
             nc.vector.quantize_mx(
@@ -239,21 +245,22 @@ def tile_qca_operator_deep_pb_s_kernel(tc, h3, w4, w5, out):
             transpose_and_copy(s)
             if s == 1:
                 multiply_zeros(BRIDGE_PASSES)
-                for a in range(PASSES):
-                    group_h3(a)
+                for b in range(BATCH):
+                    group_h3(b)
                 quantise_h3()
             if 1 <= s <= W4_SLABS:
                 quantise_slab(s - 1)
+            if s == W4_SLABS + 1:
+                quantise_h4(0)
             if s == W4_SLABS + PARTS:
                 quantise_w5(0, 0)
-                quantise_h4(0)
             for c in range(W4_LOADS):
                 if s == PAIR * c + PRODUCT_LAG:
                     multiply_zeros(KEEP_PASSES)
                     first_layer_and_exp(c)
-                if s == PAIR * (c - c // HALVES) + NEGATIVE_LAG:
+                if s == PAIR * max(c, 1) + NEGATIVE_LAG:
                     negative_branch(c)
-            if s == W4_SLABS + 1:
+            if s == W4_SLABS:
                 finish_elu(0)
             if s == W4_SLABS + PARTS:
                 quantise_w5(0, 1)

from contextlib import ExitStack

import concourse.mybir as mybir
from concourse.masks import make_identity

F32 = mybir.dt.float32
BF16 = mybir.dt.bfloat16
U32 = mybir.dt.uint32
U8 = mybir.dt.uint8
I32 = mybir.dt.int32
FP8X4 = mybir.dt.float8_e4m3fn_x4
ALU = mybir.AluOpType
ACT = mybir.ActivationFunctionType

P = 128
PACK = 4
HALVES = 2
PAIR = 2
K = 1024
PASSES = K // (P * PACK)
BATCH = 2
PIXELS_PER_IMAGE = 64
PIXELS = BATCH * PIXELS_PER_IMAGE
W4_LOADS = 4
GROUPS = 4
PARTS = 2
D = 64
W4_SLABS = W4_LOADS * PAIR
W5_PAIRS = GROUPS // PAIR
SLABS = W4_SLABS + W5_PAIRS * PARTS
TRANSPOSE_BANKS = 5
UNREAD_COLUMNS = 128
WARM_UP_PASSES = 16
BRIDGE_PASSES = 8
SHARED_SLABS = (3, 5, 7)
LAST_PASSES = 14
KEEP_PASSES = 4
NEGATIVE_LAG = 4
PRODUCT_LAG = 3

FLOPS = 2 * PIXELS * K * K + 2 * PIXELS * K * PARTS * GROUPS * D


def tile_qca_operator_deep_pb_s_kernel(tc, h3, w4, w5, out):
    nc = tc.nc
    with ExitStack() as ctx:
        keep = ctx.enter_context(tc.tile_pool(name="keep", bufs=1))
        banks = ctx.enter_context(tc.psum_pool(name="banks", bufs=TRANSPOSE_BANKS))
        h4_banks = ctx.enter_context(tc.psum_pool(name="h4_banks", bufs=1))
        out_banks = ctx.enter_context(tc.psum_pool(name="out_banks", bufs=1))
        ctx.enter_context(tc.manual_schedule())

        w4_raw = [keep.tile([P, PAIR, K], BF16, name="w4_raw%d" % c) for c in range(W4_LOADS)]
        w4_rows = w4.rearrange("(c p e) k -> c p e k", p=P, e=PAIR)
        h3_raw = keep.tile([P, BATCH, PASSES * PACK, PIXELS_PER_IMAGE], BF16)
        w5_raw = [keep.tile([P, W5_PAIRS, K], BF16, name="w5_raw%d" % h) for h in range(PARTS)]
        w5_rows = w5.rearrange("(h v p) k -> h p v k", h=PARTS, p=P)

        nc.sync.dma_start(out=w4_raw[0][:], in_=w4_rows[0])
        for b in range(BATCH):
            nc.sync.dma_start(
                out=h3_raw[:, b].rearrange("q (c e) x -> q c (e x)", e=PAIR),
                in_=h3[b].rearrange("(c q e) i j -> q c (e i j)", q=P, e=PAIR),
            )
        for c in range(1, W4_LOADS):
            nc.sync.dma_start(out=w4_raw[c][:], in_=w4_rows[c])
        nc.sync.dma_start(out=w5_raw[0][:], in_=w5_rows[0])
        for v in range(W5_PAIRS):
            nc.sync.dma_start(out=w5_raw[1][:, v, :], in_=w5_rows[1, :, v, :])

        slab_words = [w4_raw[c][:].bitcast(F32)[:, e, :] for c in range(W4_LOADS) for e in range(PAIR)]
        slab_words.extend([w5_raw[h][:].bitcast(F32)[:, v, :] for v in range(W5_PAIRS) for h in range(PARTS)])
        grouped = [
            keep.tile([P, PASSES, P, PACK], BF16, name="grouped%d" % s, align_bytes=64) for s in range(W4_SLABS)
        ]
        codes = [keep.tile([P, PASSES, P], U32, name="codes%d" % s, align_bytes=64) for s in range(W4_SLABS)]
        scales = [keep.tile([P, PASSES, P], U8, name="scales%d" % s, align_bytes=64) for s in range(W4_SLABS)]
        w5_grouped = [
            keep.tile([P, PASSES, PAIR, PARTS, D, PACK], BF16, name="w5_grouped%d" % v, align_bytes=64)
            for v in range(W5_PAIRS)
        ]
        w5_codes = [keep.tile([P, PASSES, PAIR, P], U32, name="w5_codes%d" % v, align_bytes=64) for v in range(W5_PAIRS)]
        w5_scales = [keep.tile([P, PASSES, PAIR, P], U8, name="w5_scales%d" % v, align_bytes=64) for v in range(W5_PAIRS)]

        identity = keep.tile([P, P], F32)
        make_identity(nc, identity[:])


        zeros = keep.tile([P, UNREAD_COLUMNS * PACK], BF16, align_bytes=64)
        zero_codes = keep.tile([P, UNREAD_COLUMNS], U32, align_bytes=64)
        zero_scales = keep.tile([P, UNREAD_COLUMNS], U8, align_bytes=64)
        nc.vector.memset(zeros[:].bitcast(I32), 0)
        table_warmer = keep.tile([P, 1], F32)
        nc.vector.memset(table_warmer[:], 0.0)
        nc.scalar.activation(out=table_warmer[:], in_=table_warmer[:], func=ACT.Exp)
        nc.vector.quantize_mx(out=zero_codes[:].bitcast(FP8X4), scales=zero_scales[:], in_=zeros[:])

        out_bank = out_banks.tile([P, 2 * UNREAD_COLUMNS], F32)
        out_sum = out_bank[:, 0:PIXELS]
        unread = out_bank[:, UNREAD_COLUMNS : 2 * UNREAD_COLUMNS]

        def multiply_zeros(passes):
            for i in range(passes):
                nc.tensor.matmul_mx(
                    out=unread,
                    lhsT=zero_codes[:, 0:P].bitcast(FP8X4),
                    lhsT_scale=zero_scales[:, 0:P],
                    rhs=zero_codes[:].bitcast(FP8X4),
                    rhs_scale=zero_scales[:],
                    start=True,
                    stop=True,
                )

        multiply_zeros(WARM_UP_PASSES)

        h3_grouped = keep.tile([P, PASSES, PIXELS, PACK], BF16, align_bytes=64)
        h3_codes = keep.tile([P, PASSES, PIXELS], U32, align_bytes=64)
        h3_scales = keep.tile([P, PASSES, PIXELS], U8, align_bytes=64)
        def group_h3(b):
            pixels = slice(b * PIXELS_PER_IMAGE, (b + 1) * PIXELS_PER_IMAGE)
            nc.vector.tensor_copy(
                out=h3_grouped[:, :, pixels, :], in_=h3_raw[:, b].rearrange("q (a t) x -> q a x t", t=PACK)
            )

        def quantise_h3():
            nc.vector.quantize_mx(
                out=h3_codes[:].rearrange("q a n -> q (a n)").bitcast(FP8X4),
                scales=h3_scales[:].rearrange("q a n -> q (a n)"),
                in_=h3_grouped[:].rearrange("q a n t -> q (a n t)"),
            )

        h4_sum = [h4_banks.tile([P, PACK, PIXELS], F32, name="h4_sum%d" % a) for a in range(PASSES)]
        exp_v = [keep.tile([P, PACK, PIXELS], F32, name="exp_v%d" % a) for a in range(PASSES)]
        negative = [keep.tile([P, PACK, PIXELS], F32, name="negative%d" % a) for a in range(PASSES)]
        h4_grouped = [
            keep.tile([P, PIXELS, PACK], BF16, name="h4_grouped%d" % a, align_bytes=64) for a in range(PASSES)
        ]
        h4_codes = keep.tile([P, PASSES, PIXELS], U32, align_bytes=64)
        h4_scales = keep.tile([P, PASSES, PIXELS], U8, align_bytes=64)

        def transpose_half(bank, s, a):
            for u in range(HALVES):
                first_word = (a * HALVES + u) * P
                nc.tensor.transpose(bank[:, u, a, :], slab_words[s][:, first_word : first_word + P], identity[:])

        def copy_out(copy, s, bank, passes):
            if s < W4_SLABS:
                copy(
                    out=grouped[s][:, passes].bitcast(F32),
                    in_=bank[:, :, passes, :].rearrange("q u a r -> q a r u"),
                )
            else:
                v, h = divmod(s - W4_SLABS, PARTS)
                copy(
                    out=w5_grouped[v][:, passes, :, h].bitcast(F32).rearrange("q a i d u -> q (a i) d u"),
                    in_=bank[:, :, passes, :].rearrange("q u a (i d) -> q (a i) d u", i=PAIR),
                )

        def transpose_and_copy(s):
            if s in SHARED_SLABS:
                for a, copy in enumerate((nc.scalar.copy, nc.vector.tensor_copy)):
                    bank = banks.tile([P, HALVES, PASSES, P], F32, tag="bank", name="half%d" % a)
                    transpose_half(bank, s, a)
                    copy_out(copy, s, bank, slice(a, a + 1))
            else:
                bank = banks.tile([P, HALVES, PASSES, P], F32, tag="bank")
                for a in range(PASSES):
                    transpose_half(bank, s, a)
                copy_out(nc.scalar.copy, s, bank, slice(0, PASSES))

        def quantise_slab(s):
            nc.vector.quantize_mx(
                out=codes[s][:].rearrange("q a r -> q (a r)").bitcast(FP8X4),
                scales=scales[s][:].rearrange("q a r -> q (a r)"),
                in_=grouped[s][:].rearrange("q a r t -> q (a r t)"),
            )

        def quantise_w5(v, a):
            nc.vector.quantize_mx(
                out=w5_codes[v][:, a].rearrange("q i m -> q (i m)").bitcast(FP8X4),
                scales=w5_scales[v][:, a].rearrange("q i m -> q (i m)"),
                in_=w5_grouped[v][:, a].rearrange("q i h d t -> q (i h d t)"),
            )

        def first_layer_and_exp(c):
            second_pass, u = divmod(c, HALVES)
            values = slice(u * PAIR, (u + 1) * PAIR)
            for e in range(PAIR):
                for a in range(PASSES):
                    nc.tensor.matmul_mx(
                        out=h4_sum[second_pass][:, u * PAIR + e, :],
                        lhsT=codes[c * PAIR + e][:, a, :].bitcast(FP8X4),
                        lhsT_scale=scales[c * PAIR + e][:, a, :],
                        rhs=h3_codes[:, a, :].bitcast(FP8X4),
                        rhs_scale=h3_scales[:, a, :],
                        start=(a == 0),
                        stop=(a == PASSES - 1),
                    )
            nc.scalar.activation(
                out=exp_v[second_pass][:, values, :], in_=h4_sum[second_pass][:, values, :], func=ACT.Exp
            )

        def negative_branch(c):
            second_pass, u = divmod(c, HALVES)
            values = slice(u * PAIR, (u + 1) * PAIR)
            nc.vector.tensor_scalar(
                out=negative[second_pass][:, values, :],
                in0=exp_v[second_pass][:, values, :],
                scalar1=1.0,
                scalar2=-1.0,
                op0=ALU.min,
                op1=ALU.add,
            )

        def finish_elu(second_pass):
            nc.vector.tensor_tensor(
                out=h4_grouped[second_pass][:],
                in0=negative[second_pass][:].rearrange("p t n -> p n t"),
                in1=h4_sum[second_pass][:].rearrange("p t n -> p n t"),
                op=ALU.max,
            )

        def quantise_h4(second_pass):
            nc.vector.quantize_mx(
                out=h4_codes[:, second_pass, :].bitcast(FP8X4),
                scales=h4_scales[:, second_pass, :],
                in_=h4_grouped[second_pass][:].rearrange("p n t -> p (n t)"),
            )

        out_sum_first, out_sum_last = (0, 0), (W5_PAIRS - 1, PASSES - 1)

        def second_layer(v, a):
            for i in range(PAIR):
                nc.tensor.matmul_mx(
                    out=out_sum,
                    lhsT=w5_codes[v][:, a, i, :].bitcast(FP8X4),
                    lhsT_scale=w5_scales[v][:, a, i, :],
                    rhs=h4_codes[:, a, :].bitcast(FP8X4),
                    rhs_scale=h4_scales[:, a, :],
                    start=((v, a) == out_sum_first and i == 0),
                    stop=((v, a) == out_sum_last and i == PAIR - 1),
                )

        for s in range(SLABS):
            transpose_and_copy(s)
            if s == 1:
                multiply_zeros(BRIDGE_PASSES)
                for b in range(BATCH):
                    group_h3(b)
                quantise_h3()
            if 1 <= s <= W4_SLABS:
                quantise_slab(s - 1)
            if s == W4_SLABS + 1:
                quantise_h4(0)
            if s == W4_SLABS + PARTS:
                quantise_w5(0, 0)
            for c in range(W4_LOADS):
                if s == PAIR * c + PRODUCT_LAG:
                    multiply_zeros(KEEP_PASSES)
                    first_layer_and_exp(c)
                if s == PAIR * max(c, 1) + NEGATIVE_LAG:
                    negative_branch(c)
            if s == W4_SLABS:
                finish_elu(0)
            if s == W4_SLABS + PARTS:
                quantise_w5(0, 1)
        finish_elu(1)

        multiply_zeros(LAST_PASSES)
        second_layer(0, 0)
        quantise_w5(1, 0)
        quantise_h4(1)
        second_layer(0, 1)
        second_layer(1, 0)
        quantise_w5(1, 1)
        second_layer(1, 1)

        result = keep.tile([P, PIXELS], F32)
        nc.vector.tensor_scalar_mul(out=result[:], in0=out_sum, scalar1=0.1 / GROUPS)
        nc.sync.dma_start(
            out=out.rearrange("b m i j -> m b (i j)"), in_=result[:].rearrange("m (b x) -> m b x", b=BATCH)
        )
